import numpy as np
import ml_dtypes


def mxq(x, axis, fmt="e4m3"):
    dtype, down = {"e4m3": (ml_dtypes.float8_e4m3fn, 7), "e5m2": (ml_dtypes.float8_e5m2, 14)}[fmt]
    v = np.moveaxis(np.asarray(x, np.float32).astype(ml_dtypes.bfloat16).astype(np.float64), axis, -1)
    blocks = v.reshape(v.shape[:-1] + (-1, 32))
    amax = np.abs(blocks).max(-1, keepdims=True)
    byte = np.maximum(np.where(amax > 0, np.frexp(amax)[1] - 1 + 127, 0) - down, 1)
    scale = np.exp2(byte - 127.0)
    codes = (blocks / scale).astype(np.float32).astype(dtype).astype(np.float64)
    return np.moveaxis((codes * scale).reshape(v.shape), -1, axis)


WIDE = False


def mx_kscale(k):
    if not WIDE:
        return np.ones(k)
    levels = np.array([20, -20, 10, -10, 0])
    a = np.random.permutation(np.resize(levels, k // 512 * 4)).reshape(k // 512, 4)
    idx = np.arange(k)
    return np.exp2(a[idx // 512, idx % 128 // 32])


BF16 = ml_dtypes.bfloat16


def bf(x):
    return np.asarray(x, np.float32).astype(BF16)


def f64(x):
    return np.asarray(x).astype(np.float64)


B, CB, CD, H, W = 4, 4, 512, 16, 16
C = CB * CD
T = B * H * W


def erf(a):
    a = np.clip(a, -6.0, 6.0)
    a2 = 2.0 * a * a
    term = a.copy()
    tot = a.copy()
    for n in range(1, 151):
        term = term * a2 / (2 * n + 1)
        tot = tot + term
    return 2.0 / np.sqrt(np.pi) * np.exp(-a * a) * tot


def gelu_erf(v):
    return 0.5 * v * (1.0 + erf(v / np.sqrt(2.0)))


def dgelu_erf(v):
    return 0.5 * (1.0 + erf(v / np.sqrt(2.0))) + v * np.exp(-0.5 * v * v) / np.sqrt(2.0 * np.pi)


def to_blocks(v):
    return v.transpose(1, 0, 2, 3).reshape(CB, CD, T)


def preact(x, wc):
    xb = to_blocks(x)
    mix = wc.transpose(0, 2, 1) @ xb
    mix = mix.reshape(C, B, H, W).transpose(1, 0, 2, 3)
    return x + mix


def setup_inputs():
    s = mx_kscale(T).reshape(B, 1, H, W)
    x0 = bf(np.random.standard_normal((B, C, H, W)))
    wc = bf(np.random.standard_normal((CB, CD, CD)) / np.sqrt(CD))
    g = bf(np.random.standard_normal((B, C, H, W)) * np.exp2(np.random.randint(-12, 1, (B, 1, H, W))) / s)
    z = preact(f64(x0), f64(wc))
    return {"x": bf(f64(x0) * s), "wc": wc, "z": np.asarray(z, np.float32), "grad_out": g}


def reference(x, wc, z, grad_out):
    dz = f64(grad_out) * dgelu_erf(f64(z))
    xb = to_blocks(f64(x))
    db = to_blocks(dz)
    return mxq(xb, 2, "e4m3") @ mxq(db, 2, "e5m2").transpose(0, 2, 1)

@@ -1,0 +1,228 @@
+from contextlib import ExitStack
+
+import math
+
+import concourse.masks as masks
+import concourse.mybir as mybir
+
+F32 = mybir.dt.float32
+BF16 = mybir.dt.bfloat16
+U32 = mybir.dt.uint32
+U8 = mybir.dt.uint8
+E4M3_X4 = mybir.dt.float8_e4m3fn_x4
+E5M2_X4 = mybir.dt.float8_e5m2_x4
+ACT = mybir.ActivationFunctionType
+ALU = mybir.AluOpType
+
+P = 128
+BLOCKS = 4
+BLOCK_CH = 512
+CH_PER_PART = BLOCK_CH // P
+BATCH_TOKENS = 256
+PASS_BATCHES = 2
+PASSES = 2
+PIECES = BLOCKS * PASSES
+ROW = CH_PER_PART * BATCH_TOKENS
+
+INV_SQRT_2PI = 1.0 / math.sqrt(2.0 * math.pi)
+SHIFT = 1e-15
+
+FLOPS = 2 * BLOCKS * BLOCK_CH * BLOCK_CH * PASSES * PASS_BATCHES * BATCH_TOKENS
+BYTES = BLOCKS * BLOCK_CH * 1024 * (2 + 4 + 2) + BLOCKS * BLOCK_CH * BLOCK_CH * 4
+
+
+def tile_spectralchannelmixing_v_kernel(tc, x, wc, z, grad_out, out):
+    nc = tc.nc
+    by_piece = "b (i p a) h w -> i p b (a h w)"
+    x_view = x.rearrange(by_piece, i=BLOCKS, p=P, a=CH_PER_PART)
+    z_view = z.rearrange(by_piece, i=BLOCKS, p=P, a=CH_PER_PART)
+    g_view = grad_out.rearrange(by_piece, i=BLOCKS, p=P, a=CH_PER_PART)
+
+    with ExitStack() as ctx:
+        def pool(name, bufs):
+            return ctx.enter_context(tc.tile_pool(name=name, bufs=bufs))
+
+        const = pool("const", 1)
+        x_pool = pool("x", 3)
+        z_pool = pool("z", 5)
+        g_pool = pool("g", 4)
+        gelu_pool = pool("gelu", 4)
+        rho_pool = pool("rho", 3)
+        sq_pool = pool("sq", 4)
+        dz_pool = pool("dz", 3)
+        xg_pool = pool("xg", 2)
+        dzg_pool = pool("dzg", 3)
+        keep = pool("keep", 1)
+        dq_pool = pool("dq", 2)
+        out_pool = pool("outs", 4)
+        banks = ctx.enter_context(tc.psum_pool(name="banks", bufs=4))
+        sums = ctx.enter_context(tc.psum_pool(name="sums", bufs=4))
+        ctx.enter_context(tc.manual_schedule())
+
+        ident = const.tile([P, P], F32)
+        masks.make_identity(nc, ident[:])
+        shift = const.tile([P, 1], F32)
+        nc.vector.memset(shift[:], SHIFT)
+
+        x_codes = keep.tile([P, PIECES, BLOCK_CH], U32, align_bytes=64)
+        x_scales = keep.tile([P, PIECES, BLOCK_CH], U8, align_bytes=64)
+
+        x_tiles, z_tiles, g_tiles, gelu_tiles, rho_tiles, exp_tiles = {}, {}, {}, {}, {}, {}
+        x_grouped, dz_banks, dz_grouped, dz_codes, dz_scales, acc_tiles = {}, {}, {}, {}, {}, {}
+
+        def piece_of(view, j):
+            first = PASS_BATCHES * (j % PASSES)
+            return view[j // PASSES, :, first : first + PASS_BATCHES, :]
+
+        def load_x(j):
+            x_sb = x_pool.tile([P, PASS_BATCHES, ROW], BF16)
+            nc.sync.dma_start(out=x_sb[:], in_=piece_of(x_view, j))
+            x_tiles[j] = x_sb
+
+        def load_z(j):
+            z_sb = z_pool.tile([P, PASS_BATCHES, ROW], F32)
+            nc.sync.dma_start(out=z_sb[:], in_=piece_of(z_view, j))
+            z_tiles[j] = z_sb
+
+        def load_g(j):
+            g_sb = g_pool.tile([P, PASS_BATCHES, ROW], BF16)
+            nc.sync.dma_start(out=g_sb[:], in_=piece_of(g_view, j))
+            g_tiles[j] = g_sb
+
+        def transpose_piece(piece):
+            words = piece[:].bitcast(F32)
+            pair = []
+            for half in range(2):
+                bank = banks.tile([P, 2, PASS_BATCHES, P], F32)
+                for a2 in range(2):
+                    a = 2 * half + a2
+                    for u in range(PASS_BATCHES):
+                        nc.tensor.transpose(
+                            out=bank[:, a2, u, :],
+                            in_=words[:, u, a * P : (a + 1) * P],
+                            identity=ident[:],
+                        )
+                pair.append(bank)
+            return pair
+
+        def regroup(copy, pair, grouped):
+            lines = grouped[:].bitcast(F32).rearrange("p (q h w) -> p q h w", h=2, w=4)
+            for half in range(2):
+                copy(out=lines[:, :, half, :], in_=pair[half][:].rearrange("p a u q -> p q (a u)"))
+
+        def regroup_x(j):
+            x_g = xg_pool.tile([P, 4 * BLOCK_CH], BF16, align_bytes=64)
+            regroup(nc.vector.tensor_copy, transpose_piece(x_tiles[j]), x_g)
+            x_grouped[j] = x_g
+
+        def quantise_x(j):
+            nc.vector.quantize_mx(
+                out=x_codes[:, j, :].bitcast(E4M3_X4), scales=x_scales[:, j, :], in_=x_grouped[j][:]
+            )
+
+        def scalar_functions(i):
+            pieces = range(PASSES * i, PASSES * (i + 1))
+            for j in pieces:
+                gelu = gelu_pool.tile([P, PASS_BATCHES, ROW], F32)
+                nc.scalar.activation(out=gelu[:], in_=z_tiles[j][:], func=ACT.Gelu, bias=shift[:])
+                gelu_tiles[j] = gelu
+            for j in pieces:
+                sq = sq_pool.tile([P, PASS_BATCHES, ROW], F32)
+                nc.scalar.activation(out=sq[:], in_=z_tiles[j][:], func=ACT.Square, bias=shift[:])
+                exp_tiles[j] = sq
+            for j in pieces:
+                rho = rho_pool.tile([P, PASS_BATCHES, ROW], F32)
+                nc.scalar.activation(out=rho[:], in_=exp_tiles[j][:], func=ACT.Abs_reciprocal_sqrt)
+                rho_tiles[j] = rho
+            for j in pieces:
+                sq = exp_tiles[j]
+                nc.scalar.activation(out=sq[:], in_=sq[:], func=ACT.Exp, scale=-0.5)
+
+        def phi_cdf(j):
+            t = gelu_tiles[j]
+            nc.vector.tensor_tensor(out=t[:], in0=t[:], in1=rho_tiles[j][:], op=ALU.mult)
+            nc.vector.scalar_tensor_tensor(
+                out=t[:], in0=t[:], scalar=-1.0, in1=t[:], op0=ALU.mult, op1=ALU.max
+            )
+
+        def vector_chain(j):
+            t, e = gelu_tiles[j], exp_tiles[j]
+            nc.vector.scalar_tensor_tensor(
+                out=e[:], in0=e[:], scalar=INV_SQRT_2PI, in1=z_tiles[j][:], op0=ALU.mult, op1=ALU.mult
+            )
+            nc.vector.tensor_tensor(out=t[:], in0=t[:], in1=e[:], op=ALU.add)
+            dz_sb = dz_pool.tile([P, PASS_BATCHES, ROW], BF16)
+            nc.vector.tensor_tensor(out=dz_sb[:], in0=t[:], in1=g_tiles[j][:], op=ALU.mult)
+            dz_banks[j] = transpose_piece(dz_sb)
+
+        def copy_out_dz(j):
+            dz_g = dzg_pool.tile([P, 4 * BLOCK_CH], BF16, align_bytes=64)
+            regroup(nc.scalar.copy, dz_banks[j], dz_g)
+            dz_grouped[j] = dz_g
+
+        def quantise_dz(i):
+            codes = dq_pool.tile([P, PASSES, BLOCK_CH], U32, align_bytes=64)
+            scales = dq_pool.tile([P, PASSES, BLOCK_CH], U8, align_bytes=64)
+            for c in range(PASSES):
+                nc.vector.quantize_mx(
+                    out=codes[:, c, :].bitcast(E5M2_X4),
+                    scales=scales[:, c, :],
+                    in_=dz_grouped[PASSES * i + c][:],
+                )
+            dz_codes[i], dz_scales[i] = codes, scales
+
+        def multiply(i):
+            acc_tiles[i] = []
+            for m in range(BLOCK_CH // P):
+                acc = sums.tile([P, BLOCK_CH], F32)
+                rows = slice(m * P, (m + 1) * P)
+                for c in range(PASSES):
+                    nc.tensor.matmul_mx(
+                        out=acc[:],
+                        lhsT=x_codes[:, PASSES * i + c, rows].bitcast(E4M3_X4),
+                        lhsT_scale=x_scales[:, PASSES * i + c, rows],
+                        rhs=dz_codes[i][:, c, :].bitcast(E5M2_X4),
+                        rhs_scale=dz_scales[i][:, c, :],
+                        start=(c == 0),
+                        stop=(c == PASSES - 1),
+                    )
+                acc_tiles[i].append(acc)
+
+        def store(i):
+            for m in range(BLOCK_CH // P):
+                result = out_pool.tile([P, BLOCK_CH], F32)
+                nc.scalar.copy(out=result[:], in_=acc_tiles[i][m][:])
+                nc.sync.dma_start(out=out[i, m * P : (m + 1) * P, :], in_=result[:])
+
+        load_z(0)
+        load_z(1)
+        for j in range(PIECES):
+            load_x(j)
+            regroup_x(j)
+            if j >= 1:
+                quantise_x(j - 1)
+        quantise_x(PIECES - 1)
+        for j in range(4):
+            if j >= 2:
+                load_z(j)
+            load_g(j)
+
+        for i in range(BLOCKS + 2):
+            if i < BLOCKS:
+                scalar_functions(i)
+            if 1 <= i <= BLOCKS:
+                for j in range(PASSES * (i - 1), PASSES * i):
+                    copy_out_dz(j)
+            if i < BLOCKS:
+                for j in range(PASSES * i, PASSES * (i + 1)):
+                    phi_cdf(j)
+                for j in range(PASSES * i, PASSES * (i + 1)):
+                    vector_chain(j)
+                    if j + 4 < PIECES:
+                        load_z(j + 4)
+                        load_g(j + 4)
+            if 1 <= i <= BLOCKS:
+                quantise_dz(i - 1)
+                multiply(i - 1)
+            if i >= 2:
+                store(i - 2)

@@ -23,6 +23,8 @@ PASS_BATCHES = 2
 PASSES = 2
 PIECES = BLOCKS * PASSES
 ROW = CH_PER_PART * BATCH_TOKENS
+PACK = 4
+PIECE_COLS = PACK * BLOCK_CH
 
 INV_SQRT_2PI = 1.0 / math.sqrt(2.0 * math.pi)
 SHIFT = 1e-15
@@ -33,26 +35,25 @@ BYTES = BLOCKS * BLOCK_CH * 1024 * (2 + 4 + 2) + BLOCKS * BLOCK_CH * BLOCK_CH * 
 
 def tile_spectralchannelmixing_v_kernel(tc, x, wc, z, grad_out, out):
     nc = tc.nc
-    by_piece = "b (i p a) h w -> i p b (a h w)"
-    x_view = x.rearrange(by_piece, i=BLOCKS, p=P, a=CH_PER_PART)
-    z_view = z.rearrange(by_piece, i=BLOCKS, p=P, a=CH_PER_PART)
-    g_view = grad_out.rearrange(by_piece, i=BLOCKS, p=P, a=CH_PER_PART)
+    by_piece = "b (i q a) h w -> i q b (a h w)"
+    x_view = x.rearrange(by_piece, i=BLOCKS, q=P, a=CH_PER_PART)
+    z_view = z.rearrange(by_piece, i=BLOCKS, q=P, a=CH_PER_PART)
+    g_view = grad_out.rearrange(by_piece, i=BLOCKS, q=P, a=CH_PER_PART)
+    out_view = out.rearrange("i (q a) k -> i a q k", a=CH_PER_PART)
 
     with ExitStack() as ctx:
         def pool(name, bufs):
             return ctx.enter_context(tc.tile_pool(name=name, bufs=bufs))
 
         const = pool("const", 1)
-        x_pool = pool("x", 3)
-        z_pool = pool("z", 5)
-        g_pool = pool("g", 4)
-        gelu_pool = pool("gelu", 4)
-        rho_pool = pool("rho", 3)
-        sq_pool = pool("sq", 4)
-        dz_pool = pool("dz", 3)
-        xg_pool = pool("xg", 2)
-        dzg_pool = pool("dzg", 3)
         keep = pool("keep", 1)
+        stage_pool = pool("stage", 4)
+        z_pool = pool("z", 5)
+        gelu_pool = pool("gelu", 4)
+        sq_pool = pool("sq", 4)
+        rho_pool = pool("rho", 3)
+        gt_pool = pool("gt", 4)
+        grouped_pool = pool("grouped", 3)
         dq_pool = pool("dq", 2)
         out_pool = pool("outs", 4)
         banks = ctx.enter_context(tc.psum_pool(name="banks", bufs=4))
@@ -67,76 +68,98 @@ def tile_spectralchannelmixing_v_kernel(tc, x, wc, z, grad_out, out):
         x_codes = keep.tile([P, PIECES, BLOCK_CH], U32, align_bytes=64)
         x_scales = keep.tile([P, PIECES, BLOCK_CH], U8, align_bytes=64)
 
-        x_tiles, z_tiles, g_tiles, gelu_tiles, rho_tiles, exp_tiles = {}, {}, {}, {}, {}, {}
-        x_grouped, dz_banks, dz_grouped, dz_codes, dz_scales, acc_tiles = {}, {}, {}, {}, {}, {}
+        staged_x, staged_g, z_tiles, gelu_tiles, rho_tiles, exp_tiles = {}, {}, {}, {}, {}, {}
+        g_banks, g_grouped, x_grouped, d_banks, dz_grouped, dz_codes, dz_scales, acc_tiles = {}, {}, {}, {}, {}, {}, {}, {}
+
+        def pieces_of(i):
+            return range(PASSES * i, PASSES * (i + 1))
 
         def piece_of(view, j):
             first = PASS_BATCHES * (j % PASSES)
             return view[j // PASSES, :, first : first + PASS_BATCHES, :]
-
-        def load_x(j):
-            x_sb = x_pool.tile([P, PASS_BATCHES, ROW], BF16)
-            nc.sync.dma_start(out=x_sb[:], in_=piece_of(x_view, j))
-            x_tiles[j] = x_sb
 
         def load_z(j):
             z_sb = z_pool.tile([P, PASS_BATCHES, ROW], F32)
             nc.sync.dma_start(out=z_sb[:], in_=piece_of(z_view, j))
             z_tiles[j] = z_sb
 
-        def load_g(j):
-            g_sb = g_pool.tile([P, PASS_BATCHES, ROW], BF16)
-            nc.sync.dma_start(out=g_sb[:], in_=piece_of(g_view, j))
-            g_tiles[j] = g_sb
+        def load_bf16(view, j, tiles):
+            staged = stage_pool.tile([P, PASS_BATCHES, ROW], BF16)
+            nc.sync.dma_start(out=staged[:], in_=piece_of(view, j))
+            tiles[j] = staged
 
-        def transpose_piece(piece):
-            words = piece[:].bitcast(F32)
+        def transpose_words(staged):
+            words = staged[:].bitcast(F32)
             pair = []
             for half in range(2):
-                bank = banks.tile([P, 2, PASS_BATCHES, P], F32)
+                bank = banks.tile([P, 4, P], F32)
                 for a2 in range(2):
                     a = 2 * half + a2
                     for u in range(PASS_BATCHES):
                         nc.tensor.transpose(
-                            out=bank[:, a2, u, :],
+                            out=bank[:, 2 * a2 + u, :],
                             in_=words[:, u, a * P : (a + 1) * P],
                             identity=ident[:],
                         )
                 pair.append(bank)
             return pair
 
-        def regroup(copy, pair, grouped):
-            lines = grouped[:].bitcast(F32).rearrange("p (q h w) -> p q h w", h=2, w=4)
+        def copy_words(pair, grouped):
+            halves = grouped[:].bitcast(F32).rearrange("p (h a q u) -> p h a q u", h=2, a=2, u=2)
             for half in range(2):
-                copy(out=lines[:, :, half, :], in_=pair[half][:].rearrange("p a u q -> p q (a u)"))
+                nc.vector.tensor_copy(
+                    out=halves[:, half], in_=pair[half][:].rearrange("p (a u) q -> p a q u", u=2)
+                )
 
         def regroup_x(j):
-            x_g = xg_pool.tile([P, 4 * BLOCK_CH], BF16, align_bytes=64)
-            regroup(nc.vector.tensor_copy, transpose_piece(x_tiles[j]), x_g)
+            x_g = grouped_pool.tile([P, PIECE_COLS], BF16, tag="grouped", align_bytes=64)
+            copy_words(transpose_words(staged_x[j]), x_g)
             x_grouped[j] = x_g
+
+        def transpose_g(j):
+            g_banks[j] = transpose_words(staged_g[j])
+
+        def regroup_g(j):
+            g_t = gt_pool.tile([P, PIECE_COLS], BF16)
+            copy_words(g_banks[j], g_t)
+            g_grouped[j] = g_t
 
         def quantise_x(j):
             nc.vector.quantize_mx(
                 out=x_codes[:, j, :].bitcast(E4M3_X4), scales=x_scales[:, j, :], in_=x_grouped[j][:]
             )
 
-        def scalar_functions(i):
-            pieces = range(PASSES * i, PASSES * (i + 1))
-            for j in pieces:
+        def gelus(i):
+            for j in pieces_of(i):
                 gelu = gelu_pool.tile([P, PASS_BATCHES, ROW], F32)
                 nc.scalar.activation(out=gelu[:], in_=z_tiles[j][:], func=ACT.Gelu, bias=shift[:])
                 gelu_tiles[j] = gelu
-            for j in pieces:
+
+        def squares(i):
+            for j in pieces_of(i):
                 sq = sq_pool.tile([P, PASS_BATCHES, ROW], F32)
                 nc.scalar.activation(out=sq[:], in_=z_tiles[j][:], func=ACT.Square, bias=shift[:])
                 exp_tiles[j] = sq
-            for j in pieces:
+
+        def rhos(i):
+            for j in pieces_of(i):
                 rho = rho_pool.tile([P, PASS_BATCHES, ROW], F32)
                 nc.scalar.activation(out=rho[:], in_=exp_tiles[j][:], func=ACT.Abs_reciprocal_sqrt)
                 rho_tiles[j] = rho
-            for j in pieces:
+
+        def exps(i):
+            for j in pieces_of(i):
                 sq = exp_tiles[j]
                 nc.scalar.activation(out=sq[:], in_=sq[:], func=ACT.Exp, scale=-0.5)
+
+        def store(i):
+            for m in range(CH_PER_PART):
+                result = out_pool.tile([P, BLOCK_CH], F32)
+                nc.scalar.copy(
+                    out=result[:].rearrange("p (q a) -> p q a", a=CH_PER_PART),
+                    in_=acc_tiles[i][m][:].rearrange("p (a q) -> p q a", a=CH_PER_PART),
+                )
+                nc.sync.dma_start(out=out_view[i, m], in_=result[:])
 
         def phi_cdf(j):
             t = gelu_tiles[j]
@@ -145,35 +168,57 @@ def tile_spectralchannelmixing_v_kernel(tc, x, wc, z, grad_out, out):
                 out=t[:], in0=t[:], scalar=-1.0, in1=t[:], op0=ALU.mult, op1=ALU.max
             )
 
-        def vector_chain(j):
-            t, e = gelu_tiles[j], exp_tiles[j]
+        def v_pdf(j):
+            e = exp_tiles[j]
             nc.vector.scalar_tensor_tensor(
                 out=e[:], in0=e[:], scalar=INV_SQRT_2PI, in1=z_tiles[j][:], op0=ALU.mult, op1=ALU.mult
             )
-            nc.vector.tensor_tensor(out=t[:], in0=t[:], in1=e[:], op=ALU.add)
-            dz_sb = dz_pool.tile([P, PASS_BATCHES, ROW], BF16)
-            nc.vector.tensor_tensor(out=dz_sb[:], in0=t[:], in1=g_tiles[j][:], op=ALU.mult)
-            dz_banks[j] = transpose_piece(dz_sb)
 
-        def copy_out_dz(j):
-            dz_g = dzg_pool.tile([P, 4 * BLOCK_CH], BF16, align_bytes=64)
-            regroup(nc.scalar.copy, dz_banks[j], dz_g)
+        def add_and_transpose(j):
+            d_banks[j] = []
+            for a in range(CH_PER_PART):
+                bank = banks.tile([P, 4, P], F32)
+                for u in range(PASS_BATCHES):
+                    for e in range(2):
+                        tokens = slice(a * BATCH_TOKENS + e, (a + 1) * BATCH_TOKENS, 2)
+                        for k, term in enumerate((gelu_tiles[j], exp_tiles[j])):
+                            nc.tensor.matmul(
+                                out=bank[:, 2 * u + e, :],
+                                lhsT=term[:, u, tokens],
+                                rhs=ident[:],
+                                is_transpose=True,
+                                start=(k == 0),
+                                stop=(k == 1),
+                            )
+                d_banks[j].append(bank)
+
+        def times_grad(j):
+            dz_g = grouped_pool.tile([P, PIECE_COLS], BF16, tag="grouped", align_bytes=64)
+            dz_by_a = dz_g[:].rearrange("p (a q t) -> p a q t", a=CH_PER_PART, t=PACK)
+            g_by_a = g_grouped[j][:].rearrange("p (a q t) -> p a q t", a=CH_PER_PART, t=PACK)
+            for a in range(CH_PER_PART):
+                nc.vector.tensor_tensor(
+                    out=dz_by_a[:, a],
+                    in0=d_banks[j][a][:].rearrange("p t q -> p q t"),
+                    in1=g_by_a[:, a],
+                    op=ALU.mult,
+                )
             dz_grouped[j] = dz_g
 
-        def quantise_dz(i):
-            codes = dq_pool.tile([P, PASSES, BLOCK_CH], U32, align_bytes=64)
-            scales = dq_pool.tile([P, PASSES, BLOCK_CH], U8, align_bytes=64)
-            for c in range(PASSES):
-                nc.vector.quantize_mx(
-                    out=codes[:, c, :].bitcast(E5M2_X4),
-                    scales=scales[:, c, :],
-                    in_=dz_grouped[PASSES * i + c][:],
-                )
-            dz_codes[i], dz_scales[i] = codes, scales
+        def quantise_dz(j):
+            if j % PASSES == 0:
+                codes = dq_pool.tile([P, PASSES, BLOCK_CH], U32, align_bytes=64)
+                scales = dq_pool.tile([P, PASSES, BLOCK_CH], U8, align_bytes=64)
+                dz_codes[j // PASSES], dz_scales[j // PASSES] = codes, scales
+            nc.vector.quantize_mx(
+                out=dz_codes[j // PASSES][:, j % PASSES, :].bitcast(E5M2_X4),
+                scales=dz_scales[j // PASSES][:, j % PASSES, :],
+                in_=dz_grouped[j][:],
+            )
 
         def multiply(i):
             acc_tiles[i] = []
-            for m in range(BLOCK_CH // P):
+            for m in range(CH_PER_PART):
                 acc = sums.tile([P, BLOCK_CH], F32)
                 rows = slice(m * P, (m + 1) * P)
                 for c in range(PASSES):
@@ -188,41 +233,53 @@ def tile_spectralchannelmixing_v_kernel(tc, x, wc, z, grad_out, out):
                     )
                 acc_tiles[i].append(acc)
 
-        def store(i):
-            for m in range(BLOCK_CH // P):
-                result = out_pool.tile([P, BLOCK_CH], F32)
-                nc.scalar.copy(out=result[:], in_=acc_tiles[i][m][:])
-                nc.sync.dma_start(out=out[i, m * P : (m + 1) * P, :], in_=result[:])
+        def vector_step(j):
+            if j < PIECES:
+                phi_cdf(j)
+            if j >= 1:
+                times_grad(j - 1)
+            if j + 2 < PIECES:
+                transpose_g(j + 2)
+            if j < PIECES:
+                v_pdf(j)
+            if j + 2 < PIECES:
+                regroup_g(j + 2)
+            if j < PIECES:
+                add_and_transpose(j)
+            if j + 4 < PIECES:
+                load_bf16(g_view, j + 4, staged_g)
+            if j + 5 < PIECES:
+                load_z(j + 5)
+            if j >= 1:
+                quantise_dz(j - 1)
+                if j % PASSES == 0:
+                    multiply(j // PASSES - 1)
 
-        load_z(0)
-        load_z(1)
         for j in range(PIECES):
-            load_x(j)
+            load_bf16(x_view, j, staged_x)
+            if j < 2:
+                load_z(j)
             regroup_x(j)
             if j >= 1:
                 quantise_x(j - 1)
         quantise_x(PIECES - 1)
         for j in range(4):
-            if j >= 2:
-                load_z(j)
-            load_g(j)
+            load_bf16(g_view, j, staged_g)
+            if j < 2:
+                transpose_g(j)
+                regroup_g(j)
+            if j < 3:
+                load_z(j + 2)
 
-        for i in range(BLOCKS + 2):
-            if i < BLOCKS:
-                scalar_functions(i)
-            if 1 <= i <= BLOCKS:
-                for j in range(PASSES * (i - 1), PASSES * i):
-                    copy_out_dz(j)
-            if i < BLOCKS:
-                for j in range(PASSES * i, PASSES * (i + 1)):
-                    phi_cdf(j)
-                for j in range(PASSES * i, PASSES * (i + 1)):
-                    vector_chain(j)
-                    if j + 4 < PIECES:
-                        load_z(j + 4)
-                        load_g(j + 4)
-            if 1 <= i <= BLOCKS:
-                quantise_dz(i - 1)
-                multiply(i - 1)
+        for i in range(BLOCKS):
+            gelus(i)
+            squares(i)
             if i >= 2:
                 store(i - 2)
+            rhos(i)
+            exps(i)
+            for j in pieces_of(i):
+                vector_step(j)
+        store(BLOCKS - 2)
+        vector_step(PIECES)
+        store(BLOCKS - 1)

@@ -26,7 +26,7 @@ ROW = CH_PER_PART * BATCH_TOKENS
 PACK = 4
 PIECE_COLS = PACK * BLOCK_CH
 
-INV_SQRT_2PI = 1.0 / math.sqrt(2.0 * math.pi)
+TWO_PI = 2.0 * math.pi
 SHIFT = 1e-15
 
 FLOPS = 2 * BLOCKS * BLOCK_CH * BLOCK_CH * PASSES * PASS_BATCHES * BATCH_TOKENS
@@ -129,14 +129,11 @@ def tile_spectralchannelmixing_v_kernel(tc, x, wc, z, grad_out, out):
                 out=x_codes[:, j, :].bitcast(E4M3_X4), scales=x_scales[:, j, :], in_=x_grouped[j][:]
             )
 
-        def gelus(i):
+        def gelus_and_squares(i):
             for j in pieces_of(i):
                 gelu = gelu_pool.tile([P, PASS_BATCHES, ROW], F32)
                 nc.scalar.activation(out=gelu[:], in_=z_tiles[j][:], func=ACT.Gelu, bias=shift[:])
                 gelu_tiles[j] = gelu
-
-        def squares(i):
-            for j in pieces_of(i):
                 sq = sq_pool.tile([P, PASS_BATCHES, ROW], F32)
                 nc.scalar.activation(out=sq[:], in_=z_tiles[j][:], func=ACT.Square, bias=shift[:])
                 exp_tiles[j] = sq
@@ -144,7 +141,9 @@ def tile_spectralchannelmixing_v_kernel(tc, x, wc, z, grad_out, out):
         def rhos(i):
             for j in pieces_of(i):
                 rho = rho_pool.tile([P, PASS_BATCHES, ROW], F32)
-                nc.scalar.activation(out=rho[:], in_=exp_tiles[j][:], func=ACT.Abs_reciprocal_sqrt)
+                nc.scalar.activation(
+                    out=rho[:], in_=exp_tiles[j][:], func=ACT.Abs_reciprocal_sqrt, scale=1.0 / TWO_PI
+                )
                 rho_tiles[j] = rho
 
         def exps(i):
@@ -155,7 +154,8 @@ def tile_spectralchannelmixing_v_kernel(tc, x, wc, z, grad_out, out):
         def store(i):
             for m in range(CH_PER_PART):
                 result = out_pool.tile([P, BLOCK_CH], F32)
-                nc.scalar.copy(
+                copy = nc.scalar.copy if m % 2 == 0 else nc.vector.tensor_copy
+                copy(
                     out=result[:].rearrange("p (q a) -> p q a", a=CH_PER_PART),
                     in_=acc_tiles[i][m][:].rearrange("p (a q) -> p q a", a=CH_PER_PART),
                 )
@@ -170,9 +170,7 @@ def tile_spectralchannelmixing_v_kernel(tc, x, wc, z, grad_out, out):
 
         def v_pdf(j):
             e = exp_tiles[j]
-            nc.vector.scalar_tensor_tensor(
-                out=e[:], in0=e[:], scalar=INV_SQRT_2PI, in1=z_tiles[j][:], op0=ALU.mult, op1=ALU.mult
-            )
+            nc.gpsimd.tensor_tensor(out=e[:], in0=e[:], in1=z_tiles[j][:], op=ALU.mult)
 
         def add_and_transpose(j):
             d_banks[j] = []
@@ -197,11 +195,13 @@ def tile_spectralchannelmixing_v_kernel(tc, x, wc, z, grad_out, out):
             dz_by_a = dz_g[:].rearrange("p (a q t) -> p a q t", a=CH_PER_PART, t=PACK)
             g_by_a = g_grouped[j][:].rearrange("p (a q t) -> p a q t", a=CH_PER_PART, t=PACK)
             for a in range(CH_PER_PART):
-                nc.vector.tensor_tensor(
+                nc.vector.scalar_tensor_tensor(
                     out=dz_by_a[:, a],
                     in0=d_banks[j][a][:].rearrange("p t q -> p q t"),
+                    scalar=1.0 / math.sqrt(TWO_PI),
                     in1=g_by_a[:, a],
-                    op=ALU.mult,
+                    op0=ALU.mult,
+                    op1=ALU.mult,
                 )
             dz_grouped[j] = dz_g
 
@@ -236,13 +236,11 @@ def tile_spectralchannelmixing_v_kernel(tc, x, wc, z, grad_out, out):
         def vector_step(j):
             if j < PIECES:
                 phi_cdf(j)
+                v_pdf(j)
             if j >= 1:
                 times_grad(j - 1)
             if j + 2 < PIECES:
                 transpose_g(j + 2)
-            if j < PIECES:
-                v_pdf(j)
-            if j + 2 < PIECES:
                 regroup_g(j + 2)
             if j < PIECES:
                 add_and_transpose(j)
@@ -257,8 +255,8 @@ def tile_spectralchannelmixing_v_kernel(tc, x, wc, z, grad_out, out):
 
         for j in range(PIECES):
             load_bf16(x_view, j, staged_x)
-            if j < 2:
-                load_z(j)
+            if j == 0 or j == 2:
+                load_z(j // 2)
             regroup_x(j)
             if j >= 1:
                 quantise_x(j - 1)
@@ -268,15 +266,14 @@ def tile_spectralchannelmixing_v_kernel(tc, x, wc, z, grad_out, out):
             if j < 2:
                 transpose_g(j)
                 regroup_g(j)
-            if j < 3:
-                load_z(j + 2)
+            if j >= 1:
+                load_z(j + 1)
 
         for i in range(BLOCKS):
-            gelus(i)
-            squares(i)
+            gelus_and_squares(i)
+            rhos(i)
             if i >= 2:
                 store(i - 2)
-            rhos(i)
             exps(i)
             for j in pieces_of(i):
                 vector_step(j)

@@ -25,6 +25,7 @@ PIECES = BLOCKS * PASSES
 ROW = CH_PER_PART * BATCH_TOKENS
 PACK = 4
 PIECE_COLS = PACK * BLOCK_CH
+BATCH = 3
 
 TWO_PI = 2.0 * math.pi
 SHIFT = 1e-15
@@ -47,12 +48,12 @@ def tile_spectralchannelmixing_v_kernel(tc, x, wc, z, grad_out, out):
 
         const = pool("const", 1)
         keep = pool("keep", 1)
-        stage_pool = pool("stage", 4)
-        z_pool = pool("z", 5)
-        gelu_pool = pool("gelu", 4)
-        sq_pool = pool("sq", 4)
-        rho_pool = pool("rho", 3)
-        gt_pool = pool("gt", 4)
+        stage_pool = pool("stage", 3)
+        z_pool = pool("z", 2 * BATCH)
+        gelu_pool = pool("gelu", BATCH + 2)
+        sq_pool = pool("sq", BATCH + 2)
+        rho_pool = pool("rho", BATCH)
+        gt_pool = pool("gt", 3)
         grouped_pool = pool("grouped", 3)
         dq_pool = pool("dq", 2)
         out_pool = pool("outs", 4)
@@ -69,14 +70,15 @@ def tile_spectralchannelmixing_v_kernel(tc, x, wc, z, grad_out, out):
         x_scales = keep.tile([P, PIECES, BLOCK_CH], U8, align_bytes=64)
 
         staged_x, staged_g, z_tiles, gelu_tiles, rho_tiles, exp_tiles = {}, {}, {}, {}, {}, {}
-        g_banks, g_grouped, x_grouped, d_banks, dz_grouped, dz_codes, dz_scales, acc_tiles = {}, {}, {}, {}, {}, {}, {}, {}
-
-        def pieces_of(i):
-            return range(PASSES * i, PASSES * (i + 1))
+        g_grouped, x_grouped, d_banks, dz_grouped = {}, {}, {}, {}
+        dz_codes, dz_scales, acc_tiles = {}, {}, {}
 
         def piece_of(view, j):
             first = PASS_BATCHES * (j % PASSES)
             return view[j // PASSES, :, first : first + PASS_BATCHES, :]
+
+        def channels(tile_, a):
+            return tile_[:, :, a * BATCH_TOKENS : (a + 1) * BATCH_TOKENS]
 
         def load_z(j):
             z_sb = z_pool.tile([P, PASS_BATCHES, ROW], F32)
@@ -88,9 +90,9 @@ def tile_spectralchannelmixing_v_kernel(tc, x, wc, z, grad_out, out):
             nc.sync.dma_start(out=staged[:], in_=piece_of(view, j))
             tiles[j] = staged
 
-        def transpose_words(staged):
+        def lay_out(staged, grouped):
             words = staged[:].bitcast(F32)
-            pair = []
+            halves = grouped[:].bitcast(F32).rearrange("p (h a q u) -> p h a q u", h=2, a=2, u=2)
             for half in range(2):
                 bank = banks.tile([P, 4, P], F32)
                 for a2 in range(2):
@@ -101,76 +103,55 @@ def tile_spectralchannelmixing_v_kernel(tc, x, wc, z, grad_out, out):
                             in_=words[:, u, a * P : (a + 1) * P],
                             identity=ident[:],
                         )
-                pair.append(bank)
-            return pair
-
-        def copy_words(pair, grouped):
-            halves = grouped[:].bitcast(F32).rearrange("p (h a q u) -> p h a q u", h=2, a=2, u=2)
-            for half in range(2):
                 nc.vector.tensor_copy(
-                    out=halves[:, half], in_=pair[half][:].rearrange("p (a u) q -> p a q u", u=2)
+                    out=halves[:, half], in_=bank[:].rearrange("p (a u) q -> p a q u", u=2)
                 )
 
-        def regroup_x(j):
+        def lay_out_x(j):
             x_g = grouped_pool.tile([P, PIECE_COLS], BF16, tag="grouped", align_bytes=64)
-            copy_words(transpose_words(staged_x[j]), x_g)
+            lay_out(staged_x[j], x_g)
             x_grouped[j] = x_g
-
-        def transpose_g(j):
-            g_banks[j] = transpose_words(staged_g[j])
-
-        def regroup_g(j):
-            g_t = gt_pool.tile([P, PIECE_COLS], BF16)
-            copy_words(g_banks[j], g_t)
-            g_grouped[j] = g_t
 
         def quantise_x(j):
             nc.vector.quantize_mx(
                 out=x_codes[:, j, :].bitcast(E4M3_X4), scales=x_scales[:, j, :], in_=x_grouped[j][:]
             )
 
-        def gelus_and_squares(i):
-            for j in pieces_of(i):
+        def lay_out_g(j):
+            g_t = gt_pool.tile([P, PIECE_COLS], BF16)
+            lay_out(staged_g[j], g_t)
+            g_grouped[j] = g_t
+
+        def scalar_functions(pieces):
+            for j in pieces:
                 gelu = gelu_pool.tile([P, PASS_BATCHES, ROW], F32)
                 nc.scalar.activation(out=gelu[:], in_=z_tiles[j][:], func=ACT.Gelu, bias=shift[:])
                 gelu_tiles[j] = gelu
                 sq = sq_pool.tile([P, PASS_BATCHES, ROW], F32)
                 nc.scalar.activation(out=sq[:], in_=z_tiles[j][:], func=ACT.Square, bias=shift[:])
                 exp_tiles[j] = sq
-
-        def rhos(i):
-            for j in pieces_of(i):
+            for j in pieces:
                 rho = rho_pool.tile([P, PASS_BATCHES, ROW], F32)
                 nc.scalar.activation(
                     out=rho[:], in_=exp_tiles[j][:], func=ACT.Abs_reciprocal_sqrt, scale=1.0 / TWO_PI
                 )
                 rho_tiles[j] = rho
+            for j in pieces:
+                for a in range(CH_PER_PART):
+                    sq = channels(exp_tiles[j], a)
+                    nc.scalar.activation(out=sq, in_=sq, func=ACT.Exp, scale=-0.5)
 
-        def exps(i):
-            for j in pieces_of(i):
-                sq = exp_tiles[j]
-                nc.scalar.activation(out=sq[:], in_=sq[:], func=ACT.Exp, scale=-0.5)
+        def signed_cdf(j):
+            for a in range(CH_PER_PART):
+                t = channels(gelu_tiles[j], a)
+                nc.gpsimd.tensor_tensor(out=t, in0=t, in1=channels(rho_tiles[j], a), op=ALU.mult)
 
-        def store(i):
-            for m in range(CH_PER_PART):
-                result = out_pool.tile([P, BLOCK_CH], F32)
-                copy = nc.scalar.copy if m % 2 == 0 else nc.vector.tensor_copy
-                copy(
-                    out=result[:].rearrange("p (q a) -> p q a", a=CH_PER_PART),
-                    in_=acc_tiles[i][m][:].rearrange("p (a q) -> p q a", a=CH_PER_PART),
-                )
-                nc.sync.dma_start(out=out_view[i, m], in_=result[:])
-
-        def phi_cdf(j):
-            t = gelu_tiles[j]
-            nc.vector.tensor_tensor(out=t[:], in0=t[:], in1=rho_tiles[j][:], op=ALU.mult)
-            nc.vector.scalar_tensor_tensor(
-                out=t[:], in0=t[:], scalar=-1.0, in1=t[:], op0=ALU.mult, op1=ALU.max
-            )
-
-        def v_pdf(j):
-            e = exp_tiles[j]
-            nc.gpsimd.tensor_tensor(out=e[:], in0=e[:], in1=z_tiles[j][:], op=ALU.mult)
+        def gelu_terms(j):
+            for a in range(CH_PER_PART):
+                t = channels(gelu_tiles[j], a)
+                nc.vector.scalar_tensor_tensor(out=t, in0=t, scalar=-1.0, in1=t, op0=ALU.mult, op1=ALU.max)
+                e = channels(exp_tiles[j], a)
+                nc.vector.tensor_tensor(out=e, in0=e, in1=channels(z_tiles[j], a), op=ALU.mult)
 
         def add_and_transpose(j):
             d_banks[j] = []
@@ -206,14 +187,13 @@ def tile_spectralchannelmixing_v_kernel(tc, x, wc, z, grad_out, out):
             dz_grouped[j] = dz_g
 
         def quantise_dz(j):
-            if j % PASSES == 0:
+            i, c = divmod(j, PASSES)
+            if c == 0:
                 codes = dq_pool.tile([P, PASSES, BLOCK_CH], U32, align_bytes=64)
                 scales = dq_pool.tile([P, PASSES, BLOCK_CH], U8, align_bytes=64)
-                dz_codes[j // PASSES], dz_scales[j // PASSES] = codes, scales
+                dz_codes[i], dz_scales[i] = codes, scales
             nc.vector.quantize_mx(
-                out=dz_codes[j // PASSES][:, j % PASSES, :].bitcast(E5M2_X4),
-                scales=dz_scales[j // PASSES][:, j % PASSES, :],
-                in_=dz_grouped[j][:],
+                out=dz_codes[i][:, c, :].bitcast(E5M2_X4), scales=dz_scales[i][:, c, :], in_=dz_grouped[j][:]
             )
 
         def multiply(i):
@@ -233,50 +213,70 @@ def tile_spectralchannelmixing_v_kernel(tc, x, wc, z, grad_out, out):
                     )
                 acc_tiles[i].append(acc)
 
-        def vector_step(j):
+        def store(i, copies):
+            for m in range(CH_PER_PART):
+                result = out_pool.tile([P, BLOCK_CH], F32)
+                copies[m % len(copies)](
+                    out=result[:].rearrange("p (q a) -> p q a", a=CH_PER_PART),
+                    in_=acc_tiles[i][m][:].rearrange("p (a q) -> p q a", a=CH_PER_PART),
+                )
+                nc.sync.dma_start(out=out_view[i, m], in_=result[:])
+
+        def retire(j):
+            if j >= 0:
+                times_grad(j)
+            if j + 3 < PIECES:
+                lay_out_g(j + 3)
+
+        def hand_over(j):
+            if j < 0:
+                return
+            quantise_dz(j)
+            if j % PASSES == 1:
+                multiply(j // PASSES)
+            elif j >= PASSES:
+                store(j // PASSES - 1, [nc.vector.tensor_copy])
+
+        def vector_step(j, waits_for_scalar):
+            if waits_for_scalar:
+                retire(j - 1)
+                hand_over(j - 1)
             if j < PIECES:
-                phi_cdf(j)
-                v_pdf(j)
-            if j >= 1:
-                times_grad(j - 1)
-            if j + 2 < PIECES:
-                transpose_g(j + 2)
-                regroup_g(j + 2)
+                gelu_terms(j)
+            if not waits_for_scalar:
+                retire(j - 1)
             if j < PIECES:
                 add_and_transpose(j)
             if j + 4 < PIECES:
                 load_bf16(g_view, j + 4, staged_g)
-            if j + 5 < PIECES:
-                load_z(j + 5)
-            if j >= 1:
-                quantise_dz(j - 1)
-                if j % PASSES == 0:
-                    multiply(j // PASSES - 1)
+            if j + 2 * BATCH < PIECES:
+                load_z(j + 2 * BATCH)
+            if not waits_for_scalar:
+                hand_over(j - 1)
 
+        load_z(0)
         for j in range(PIECES):
             load_bf16(x_view, j, staged_x)
-            if j == 0 or j == 2:
-                load_z(j // 2)
-            regroup_x(j)
+            if j % 2 == 1 and j // 2 + 1 < BATCH:
+                load_z(j // 2 + 1)
+            lay_out_x(j)
             if j >= 1:
                 quantise_x(j - 1)
         quantise_x(PIECES - 1)
         for j in range(4):
             load_bf16(g_view, j, staged_g)
             if j < 2:
-                transpose_g(j)
-                regroup_g(j)
-            if j >= 1:
+                lay_out_g(j)
+            else:
                 load_z(j + 1)
+        load_z(2 * BATCH - 1)
 
-        for i in range(BLOCKS):
-            gelus_and_squares(i)
-            rhos(i)
-            if i >= 2:
-                store(i - 2)
-            exps(i)
-            for j in pieces_of(i):
-                vector_step(j)
-        store(BLOCKS - 2)
-        vector_step(PIECES)
-        store(BLOCKS - 1)
+        for first in range(0, PIECES, BATCH):
+            pieces = range(first, min(first + BATCH, PIECES))
+            scalar_functions(pieces)
+            for j in pieces:
+                signed_cdf(j)
+            for j in pieces:
+                vector_step(j, j == first)
+        vector_step(PIECES, True)
+        store(BLOCKS - 1, [nc.scalar.copy, nc.vector.tensor_copy])

@@ -80,6 +80,9 @@ def tile_spectralchannelmixing_v_kernel(tc, x, wc, z, grad_out, out):
         def channels(tile_, a):
             return tile_[:, :, a * BATCH_TOKENS : (a + 1) * BATCH_TOKENS]
 
+        def sorted_tokens(natural):
+            return natural.rearrange("q r (p e) -> q r e p", e=2)
+
         def load_z(j):
             z_sb = z_pool.tile([P, PASS_BATCHES, ROW], F32)
             nc.sync.dma_start(out=z_sb[:], in_=piece_of(z_view, j))
@@ -124,11 +127,24 @@ def tile_spectralchannelmixing_v_kernel(tc, x, wc, z, grad_out, out):
 
         def scalar_functions(pieces):
             for j in pieces:
+                by_set = "q u (a t) -> q (u a) t"
+                v = sorted_tokens(z_tiles[j][:].rearrange(by_set, a=CH_PER_PART))
+                split = "q r (e p) -> q r e p"
                 gelu = gelu_pool.tile([P, PASS_BATCHES, ROW], F32)
-                nc.scalar.activation(out=gelu[:], in_=z_tiles[j][:], func=ACT.Gelu, bias=shift[:])
+                nc.scalar.activation(
+                    out=gelu[:].rearrange(by_set, a=CH_PER_PART).rearrange(split, e=2),
+                    in_=v,
+                    func=ACT.Gelu,
+                    bias=shift[:],
+                )
                 gelu_tiles[j] = gelu
                 sq = sq_pool.tile([P, PASS_BATCHES, ROW], F32)
-                nc.scalar.activation(out=sq[:], in_=z_tiles[j][:], func=ACT.Square, bias=shift[:])
+                nc.scalar.activation(
+                    out=sq[:].rearrange(by_set, a=CH_PER_PART).rearrange(split, e=2),
+                    in_=v,
+                    func=ACT.Square,
+                    bias=shift[:],
+                )
                 exp_tiles[j] = sq
             for j in pieces:
                 rho = rho_pool.tile([P, PASS_BATCHES, ROW], F32)
@@ -150,8 +166,10 @@ def tile_spectralchannelmixing_v_kernel(tc, x, wc, z, grad_out, out):
             for a in range(CH_PER_PART):
                 t = channels(gelu_tiles[j], a)
                 nc.vector.scalar_tensor_tensor(out=t, in0=t, scalar=-1.0, in1=t, op0=ALU.mult, op1=ALU.max)
-                e = channels(exp_tiles[j], a)
-                nc.vector.tensor_tensor(out=e, in0=e, in1=channels(z_tiles[j], a), op=ALU.mult)
+                e = channels(exp_tiles[j], a).rearrange("q r (e p) -> q r e p", e=2)
+                nc.vector.tensor_tensor(
+                    out=e, in0=e, in1=sorted_tokens(channels(z_tiles[j], a)), op=ALU.mult
+                )
 
         def add_and_transpose(j):
             d_banks[j] = []
@@ -159,7 +177,8 @@ def tile_spectralchannelmixing_v_kernel(tc, x, wc, z, grad_out, out):
                 bank = banks.tile([P, 4, P], F32)
                 for u in range(PASS_BATCHES):
                     for e in range(2):
-                        tokens = slice(a * BATCH_TOKENS + e, (a + 1) * BATCH_TOKENS, 2)
+                        first = a * BATCH_TOKENS + e * P
+                        tokens = slice(first, first + P)
                         for k, term in enumerate((gelu_tiles[j], exp_tiles[j])):
                             nc.tensor.matmul(
                                 out=bank[:, 2 * u + e, :],

@@ -25,10 +25,10 @@ PIECES = BLOCKS * PASSES
 ROW = CH_PER_PART * BATCH_TOKENS
 PACK = 4
 PIECE_COLS = PACK * BLOCK_CH
-BATCH = 3
+HALF = PIECES // 2
 
-TWO_PI = 2.0 * math.pi
-SHIFT = 1e-15
+SHIFT = 2.0**-56
+LOG_PHI0 = -0.5 * math.log(2.0 * math.pi)
 
 FLOPS = 2 * BLOCKS * BLOCK_CH * BLOCK_CH * PASSES * PASS_BATCHES * BATCH_TOKENS
 BYTES = BLOCKS * BLOCK_CH * 1024 * (2 + 4 + 2) + BLOCKS * BLOCK_CH * BLOCK_CH * 4
@@ -48,30 +48,36 @@ def tile_spectralchannelmixing_v_kernel(tc, x, wc, z, grad_out, out):
 
         const = pool("const", 1)
         keep = pool("keep", 1)
-        stage_pool = pool("stage", 3)
-        z_pool = pool("z", 2 * BATCH)
-        gelu_pool = pool("gelu", BATCH + 2)
-        sq_pool = pool("sq", BATCH + 2)
-        rho_pool = pool("rho", BATCH)
-        gt_pool = pool("gt", 3)
+        x_pool = pool("xs", 2)
+        g_pool = pool("gs", 4)
+        z_pool = pool("z", 8)
+        sq_pool = pool("sq", 4)
+        exp_pool = pool("exps", 4)
+        rho_pool = pool("rho", 4)
+        sign_pool = pool("signs", 2)
         grouped_pool = pool("grouped", 3)
         dq_pool = pool("dq", 2)
         out_pool = pool("outs", 4)
-        banks = ctx.enter_context(tc.psum_pool(name="banks", bufs=4))
-        sums = ctx.enter_context(tc.psum_pool(name="sums", bufs=4))
-        ctx.enter_context(tc.manual_schedule())
+        q_banks = ctx.enter_context(tc.psum_pool(name="q_banks", bufs=2))
+        banks = ctx.enter_context(tc.psum_pool(name="banks", bufs=2))
+        s_banks = ctx.enter_context(tc.psum_pool(name="s_banks", bufs=2))
+        sums = ctx.enter_context(tc.psum_pool(name="sums", bufs=2))
+        ctx.enter_context(tc.manual_schedule(engines={mybir.EngineType.Activation, mybir.EngineType.SP}))
 
-        ident = const.tile([P, P], F32)
-        masks.make_identity(nc, ident[:])
         shift = const.tile([P, 1], F32)
         nc.vector.memset(shift[:], SHIFT)
+        floor = const.tile([P, 1], F32)
+        nc.vector.memset(floor[:], SHIFT * SHIFT / 4.0)
+        warm = const.tile([P, 1], F32)
+        nc.scalar.activation(out=warm[:], in_=shift[:], func=ACT.Abs_reciprocal_sqrt)
+        ident = const.tile([P, P], F32)
+        masks.make_identity(nc, ident[:])
 
         x_codes = keep.tile([P, PIECES, BLOCK_CH], U32, align_bytes=64)
         x_scales = keep.tile([P, PIECES, BLOCK_CH], U8, align_bytes=64)
 
-        staged_x, staged_g, z_tiles, gelu_tiles, rho_tiles, exp_tiles = {}, {}, {}, {}, {}, {}
-        g_grouped, x_grouped, d_banks, dz_grouped = {}, {}, {}, {}
-        dz_codes, dz_scales, acc_tiles = {}, {}, {}
+        staged_x, staged_g, z_tiles, sq_tiles, exp_tiles, rho_tiles = {}, {}, {}, {}, {}, {}
+        x_grouped, dz_grouped, dz_codes, dz_scales = {}, {}, {}, {}
 
         def piece_of(view, j):
             first = PASS_BATCHES * (j % PASSES)
@@ -83,36 +89,42 @@ def tile_spectralchannelmixing_v_kernel(tc, x, wc, z, grad_out, out):
         def sorted_tokens(natural):
             return natural.rearrange("q r (p e) -> q r e p", e=2)
 
+        def split(tile_):
+            return tile_.rearrange("q r (e p) -> q r e p", e=2)
+
         def load_z(j):
             z_sb = z_pool.tile([P, PASS_BATCHES, ROW], F32)
-            nc.sync.dma_start(out=z_sb[:], in_=piece_of(z_view, j))
+            for u in range(PASS_BATCHES):
+                nc.sync.dma_start(out=z_sb[:, u], in_=piece_of(z_view, j)[:, u])
             z_tiles[j] = z_sb
 
-        def load_bf16(view, j, tiles):
-            staged = stage_pool.tile([P, PASS_BATCHES, ROW], BF16)
-            nc.sync.dma_start(out=staged[:], in_=piece_of(view, j))
-            tiles[j] = staged
+        def load_x(j):
+            x_sb = x_pool.tile([P, PASS_BATCHES, ROW], BF16)
+            nc.sync.dma_start(out=x_sb[:], in_=piece_of(x_view, j))
+            staged_x[j] = x_sb
 
-        def lay_out(staged, grouped):
+        def load_g(j):
+            g_sb = g_pool.tile([P, PASS_BATCHES, ROW], BF16)
+            nc.sync.dma_start(out=g_sb[:], in_=piece_of(g_view, j))
+            staged_g[j] = g_sb
+
+        def transpose_words(staged, half):
             words = staged[:].bitcast(F32)
-            halves = grouped[:].bitcast(F32).rearrange("p (h a q u) -> p h a q u", h=2, a=2, u=2)
-            for half in range(2):
-                bank = banks.tile([P, 4, P], F32)
-                for a2 in range(2):
-                    a = 2 * half + a2
-                    for u in range(PASS_BATCHES):
-                        nc.tensor.transpose(
-                            out=bank[:, 2 * a2 + u, :],
-                            in_=words[:, u, a * P : (a + 1) * P],
-                            identity=ident[:],
-                        )
-                nc.vector.tensor_copy(
-                    out=halves[:, half], in_=bank[:].rearrange("p (a u) q -> p a q u", u=2)
-                )
+            bank = banks.tile([P, 4, P], F32)
+            for a2 in range(2):
+                a = 2 * half + a2
+                for u in range(PASS_BATCHES):
+                    nc.tensor.transpose(
+                        out=bank[:, 2 * a2 + u, :], in_=words[:, u, a * P : (a + 1) * P], identity=ident[:]
+                    )
+            return bank
 
-        def lay_out_x(j):
+        def lay_out_x(j, copy):
             x_g = grouped_pool.tile([P, PIECE_COLS], BF16, tag="grouped", align_bytes=64)
-            lay_out(staged_x[j], x_g)
+            halves = x_g[:].bitcast(F32).rearrange("p (h a q u) -> p h a q u", h=2, a=2, u=2)
+            for half in range(2):
+                bank = transpose_words(staged_x[j], half)
+                copy(out=halves[:, half], in_=bank[:].rearrange("p (a u) q -> p a q u", u=2))
             x_grouped[j] = x_g
 
         def quantise_x(j):
@@ -120,88 +132,104 @@ def tile_spectralchannelmixing_v_kernel(tc, x, wc, z, grad_out, out):
                 out=x_codes[:, j, :].bitcast(E4M3_X4), scales=x_scales[:, j, :], in_=x_grouped[j][:]
             )
 
-        def lay_out_g(j):
-            g_t = gt_pool.tile([P, PIECE_COLS], BF16)
-            lay_out(staged_g[j], g_t)
-            g_grouped[j] = g_t
+        def gelu_of(j):
+            for a in range(CH_PER_PART):
+                v = channels(z_tiles[j], a)
+                nc.scalar.activation(out=v, in_=v, func=ACT.Gelu, bias=shift[:])
 
-        def scalar_functions(pieces):
-            for j in pieces:
-                by_set = "q u (a t) -> q (u a) t"
-                v = sorted_tokens(z_tiles[j][:].rearrange(by_set, a=CH_PER_PART))
-                split = "q r (e p) -> q r e p"
-                gelu = gelu_pool.tile([P, PASS_BATCHES, ROW], F32)
+        def gp_square_of(j):
+            sq = sq_pool.tile([P, PASS_BATCHES, ROW], F32)
+            for a in range(CH_PER_PART):
+                v = sorted_tokens(channels(z_tiles[j], a))
+                nc.gpsimd.tensor_tensor(out=split(channels(sq, a)), in0=v, in1=v, op=ALU.mult)
+            sq_tiles[j] = sq
+
+        def square_of(j):
+            sq = sq_pool.tile([P, PASS_BATCHES, ROW], F32)
+            for u in range(PASS_BATCHES):
                 nc.scalar.activation(
-                    out=gelu[:].rearrange(by_set, a=CH_PER_PART).rearrange(split, e=2),
-                    in_=v,
-                    func=ACT.Gelu,
-                    bias=shift[:],
-                )
-                gelu_tiles[j] = gelu
-                sq = sq_pool.tile([P, PASS_BATCHES, ROW], F32)
-                nc.scalar.activation(
-                    out=sq[:].rearrange(by_set, a=CH_PER_PART).rearrange(split, e=2),
-                    in_=v,
+                    out=split(sq[:, u].rearrange("q (a t) -> q a t", a=CH_PER_PART)),
+                    in_=sorted_tokens(z_tiles[j][:, u].rearrange("q (a t) -> q a t", a=CH_PER_PART)),
                     func=ACT.Square,
-                    bias=shift[:],
                 )
-                exp_tiles[j] = sq
-            for j in pieces:
-                rho = rho_pool.tile([P, PASS_BATCHES, ROW], F32)
-                nc.scalar.activation(
-                    out=rho[:], in_=exp_tiles[j][:], func=ACT.Abs_reciprocal_sqrt, scale=1.0 / TWO_PI
+            sq_tiles[j] = sq
+
+        def signed_grad(j):
+            signs = []
+            for u in range(PASS_BATCHES):
+                s = sign_pool.tile([P, ROW], BF16)
+                nc.vector.tensor_scalar(
+                    out=s[:], in0=z_tiles[j][:, u], scalar1=-SHIFT, scalar2=0.5, op0=ALU.is_ge, op1=ALU.subtract
                 )
-                rho_tiles[j] = rho
-            for j in pieces:
-                for a in range(CH_PER_PART):
-                    sq = channels(exp_tiles[j], a)
-                    nc.scalar.activation(out=sq, in_=sq, func=ACT.Exp, scale=-0.5)
+                signs.append(s)
+            for u in range(PASS_BATCHES):
+                g = staged_g[j][:, u]
+                nc.vector.tensor_tensor(out=g, in0=g, in1=signs[u][:], op=ALU.mult)
 
-        def signed_cdf(j):
+        def reciprocal_of(j):
+            rho = rho_pool.tile([P, PIECE_COLS], F32)
+            by_a = rho[:].rearrange("p (a q t) -> p a q t", a=CH_PER_PART, t=PACK)
             for a in range(CH_PER_PART):
-                t = channels(gelu_tiles[j], a)
-                nc.gpsimd.tensor_tensor(out=t, in0=t, in1=channels(rho_tiles[j], a), op=ALU.mult)
-
-        def gelu_terms(j):
-            for a in range(CH_PER_PART):
-                t = channels(gelu_tiles[j], a)
-                nc.vector.scalar_tensor_tensor(out=t, in0=t, scalar=-1.0, in1=t, op0=ALU.mult, op1=ALU.max)
-                e = channels(exp_tiles[j], a).rearrange("q r (e p) -> q r e p", e=2)
-                nc.vector.tensor_tensor(
-                    out=e, in0=e, in1=sorted_tokens(channels(z_tiles[j], a)), op=ALU.mult
-                )
-
-        def add_and_transpose(j):
-            d_banks[j] = []
-            for a in range(CH_PER_PART):
-                bank = banks.tile([P, 4, P], F32)
+                bank = q_banks.tile([P, 4, P], F32)
                 for u in range(PASS_BATCHES):
                     for e in range(2):
                         first = a * BATCH_TOKENS + e * P
-                        tokens = slice(first, first + P)
-                        for k, term in enumerate((gelu_tiles[j], exp_tiles[j])):
+                        nc.tensor.transpose(
+                            out=bank[:, 2 * u + e, :], in_=sq_tiles[j][:, u, first : first + P], identity=ident[:]
+                        )
+                nc.scalar.activation(
+                    out=by_a[:, a],
+                    in_=bank[:].rearrange("p t q -> p q t"),
+                    func=ACT.Abs_reciprocal_sqrt,
+                    scale=0.25,
+                    bias=floor[:],
+                )
+            rho_tiles[j] = rho
+
+        def grad_over_v(j):
+            by_a = rho_tiles[j][:].rearrange("p (a q u e) -> p a q u e", a=CH_PER_PART, u=2, e=2)
+            for half in range(2):
+                bank = transpose_words(staged_g[j], half)
+                signed = bank[:].bitcast(BF16).rearrange("p (a u) (q e) -> p a q u e", u=2, e=2)
+                for a2 in range(2):
+                    f = by_a[:, 2 * half + a2]
+                    nc.vector.tensor_tensor(out=f, in0=signed[:, a2], in1=f, op=ALU.mult)
+
+        def exp_of(j):
+            e_t = exp_pool.tile([P, PASS_BATCHES, ROW], F32)
+            for a in range(CH_PER_PART):
+                nc.scalar.activation(
+                    out=channels(e_t, a), in_=channels(sq_tiles[j], a), func=ACT.Exp, scale=-0.5, bias=LOG_PHI0
+                )
+            exp_tiles[j] = e_t
+
+        def square_times_phi(j):
+            for a in range(CH_PER_PART):
+                e_t = channels(exp_tiles[j], a)
+                nc.gpsimd.tensor_tensor(out=e_t, in0=e_t, in1=channels(sq_tiles[j], a), op=ALU.mult)
+
+        def gradient(j):
+            dz_g = grouped_pool.tile([P, PIECE_COLS], BF16, tag="grouped", align_bytes=64)
+            dz_by_a = dz_g[:].rearrange("p (a q t) -> p a q t", a=CH_PER_PART, t=PACK)
+            f_by_a = rho_tiles[j][:].rearrange("p (a q t) -> p a q t", a=CH_PER_PART, t=PACK)
+            for a in range(CH_PER_PART):
+                bank = s_banks.tile([P, 4, P], F32)
+                for u in range(PASS_BATCHES):
+                    for e in range(2):
+                        first = a * BATCH_TOKENS
+                        gelu = z_tiles[j][:, u, first + e : first + BATCH_TOKENS : 2]
+                        w = exp_tiles[j][:, u, first + e * P : first + (e + 1) * P]
+                        for k, term in enumerate((gelu, w)):
                             nc.tensor.matmul(
                                 out=bank[:, 2 * u + e, :],
-                                lhsT=term[:, u, tokens],
+                                lhsT=term,
                                 rhs=ident[:],
                                 is_transpose=True,
                                 start=(k == 0),
                                 stop=(k == 1),
                             )
-                d_banks[j].append(bank)
-
-        def times_grad(j):
-            dz_g = grouped_pool.tile([P, PIECE_COLS], BF16, tag="grouped", align_bytes=64)
-            dz_by_a = dz_g[:].rearrange("p (a q t) -> p a q t", a=CH_PER_PART, t=PACK)
-            g_by_a = g_grouped[j][:].rearrange("p (a q t) -> p a q t", a=CH_PER_PART, t=PACK)
-            for a in range(CH_PER_PART):
-                nc.vector.scalar_tensor_tensor(
-                    out=dz_by_a[:, a],
-                    in0=d_banks[j][a][:].rearrange("p t q -> p q t"),
-                    scalar=1.0 / math.sqrt(TWO_PI),
-                    in1=g_by_a[:, a],
-                    op0=ALU.mult,
-                    op1=ALU.mult,
+                nc.vector.tensor_tensor(
+                    out=dz_by_a[:, a], in0=bank[:].rearrange("p t q -> p q t"), in1=f_by_a[:, a], op=ALU.mult
                 )
             dz_grouped[j] = dz_g
 
@@ -215,87 +243,153 @@ def tile_spectralchannelmixing_v_kernel(tc, x, wc, z, grad_out, out):
                 out=dz_codes[i][:, c, :].bitcast(E5M2_X4), scales=dz_scales[i][:, c, :], in_=dz_grouped[j][:]
             )
 
-        def multiply(i):
-            acc_tiles[i] = []
-            for m in range(CH_PER_PART):
-                acc = sums.tile([P, BLOCK_CH], F32)
-                rows = slice(m * P, (m + 1) * P)
-                for c in range(PASSES):
-                    nc.tensor.matmul_mx(
-                        out=acc[:],
-                        lhsT=x_codes[:, PASSES * i + c, rows].bitcast(E4M3_X4),
-                        lhsT_scale=x_scales[:, PASSES * i + c, rows],
-                        rhs=dz_codes[i][:, c, :].bitcast(E5M2_X4),
-                        rhs_scale=dz_scales[i][:, c, :],
-                        start=(c == 0),
-                        stop=(c == PASSES - 1),
-                    )
-                acc_tiles[i].append(acc)
-
-        def store(i, copies):
-            for m in range(CH_PER_PART):
-                result = out_pool.tile([P, BLOCK_CH], F32)
-                copies[m % len(copies)](
-                    out=result[:].rearrange("p (q a) -> p q a", a=CH_PER_PART),
-                    in_=acc_tiles[i][m][:].rearrange("p (a q) -> p q a", a=CH_PER_PART),
+        def product(i, m):
+            acc = sums.tile([P, BLOCK_CH], F32)
+            rows = slice(m * P, (m + 1) * P)
+            for c in range(PASSES):
+                nc.tensor.matmul_mx(
+                    out=acc[:],
+                    lhsT=x_codes[:, PASSES * i + c, rows].bitcast(E4M3_X4),
+                    lhsT_scale=x_scales[:, PASSES * i + c, rows],
+                    rhs=dz_codes[i][:, c, :].bitcast(E5M2_X4),
+                    rhs_scale=dz_scales[i][:, c, :],
+                    start=(c == 0),
+                    stop=(c == PASSES - 1),
                 )
-                nc.sync.dma_start(out=out_view[i, m], in_=result[:])
+            return acc
 
-        def retire(j):
-            if j >= 0:
-                times_grad(j)
-            if j + 3 < PIECES:
-                lay_out_g(j + 3)
+        def store(i, m, acc, copy):
+            result = out_pool.tile([P, BLOCK_CH], F32)
+            copy(
+                out=result[:].rearrange("p (q a) -> p q a", a=CH_PER_PART),
+                in_=acc[:].rearrange("p (a q) -> p q a", a=CH_PER_PART),
+            )
+            nc.sync.dma_start(out=out_view[i, m], in_=result[:])
 
-        def hand_over(j):
-            if j < 0:
-                return
-            quantise_dz(j)
-            if j % PASSES == 1:
-                multiply(j // PASSES)
-            elif j >= PASSES:
-                store(j // PASSES - 1, [nc.vector.tensor_copy])
+        def finish(i, copies):
+            accs = [product(i, 0)]
+            for m in range(CH_PER_PART):
+                if m + 1 < CH_PER_PART:
+                    accs.append(product(i, m + 1))
+                store(i, m, accs[m], copies[m % len(copies)])
 
-        def vector_step(j, waits_for_scalar):
-            if waits_for_scalar:
-                retire(j - 1)
-                hand_over(j - 1)
-            if j < PIECES:
-                gelu_terms(j)
-            if not waits_for_scalar:
-                retire(j - 1)
-            if j < PIECES:
-                add_and_transpose(j)
-            if j + 4 < PIECES:
-                load_bf16(g_view, j + 4, staged_g)
-            if j + 2 * BATCH < PIECES:
-                load_z(j + 2 * BATCH)
-            if not waits_for_scalar:
-                hand_over(j - 1)
+        first_half = range(HALF)
+        second_half = range(HALF, PIECES)
 
+        vc, sc = nc.vector.tensor_copy, nc.scalar.copy
         load_z(0)
-        for j in range(PIECES):
-            load_bf16(x_view, j, staged_x)
-            if j % 2 == 1 and j // 2 + 1 < BATCH:
-                load_z(j // 2 + 1)
-            lay_out_x(j)
-            if j >= 1:
-                quantise_x(j - 1)
-        quantise_x(PIECES - 1)
-        for j in range(4):
-            load_bf16(g_view, j, staged_g)
-            if j < 2:
-                lay_out_g(j)
-            else:
-                load_z(j + 1)
-        load_z(2 * BATCH - 1)
-
-        for first in range(0, PIECES, BATCH):
-            pieces = range(first, min(first + BATCH, PIECES))
-            scalar_functions(pieces)
-            for j in pieces:
-                signed_cdf(j)
-            for j in pieces:
-                vector_step(j, j == first)
-        vector_step(PIECES, True)
-        store(BLOCKS - 1, [nc.scalar.copy, nc.vector.tensor_copy])
+        load_x(0)
+        load_z(1)
+        square_of(0)
+        lay_out_x(0, vc)
+        gp_square_of(1)
+        load_x(1)
+        load_g(0)
+        load_z(2)
+        reciprocal_of(0)
+        lay_out_x(1, vc)
+        quantise_x(0)
+        signed_grad(0)
+        square_of(2)
+        reciprocal_of(1)
+        load_z(3)
+        grad_over_v(0)
+        load_g(1)
+        load_x(2)
+        lay_out_x(2, vc)
+        quantise_x(1)
+        signed_grad(1)
+        gp_square_of(3)
+        reciprocal_of(2)
+        grad_over_v(1)
+        load_g(2)
+        load_x(3)
+        reciprocal_of(3)
+        signed_grad(2)
+        grad_over_v(2)
+        load_g(3)
+        signed_grad(3)
+        grad_over_v(3)
+        load_z(4)
+        lay_out_x(3, vc)
+        quantise_x(2)
+        gelu_of(0)
+        gelu_of(1)
+        gelu_of(2)
+        gelu_of(3)
+        load_x(4)
+        lay_out_x(4, vc)
+        quantise_x(3)
+        load_z(5)
+        exp_of(0)
+        square_times_phi(0)
+        exp_of(1)
+        square_times_phi(1)
+        exp_of(2)
+        square_times_phi(2)
+        exp_of(3)
+        square_times_phi(3)
+        square_of(4)
+        exp_of(4)
+        square_times_phi(4)
+        load_g(4)
+        load_x(5)
+        lay_out_x(5, vc)
+        quantise_x(4)
+        gradient(0)
+        load_x(6)
+        lay_out_x(6, vc)
+        quantise_x(5)
+        gradient(1)
+        quantise_dz(0)
+        load_x(7)
+        load_z(6)
+        lay_out_x(7, vc)
+        quantise_x(6)
+        quantise_x(7)
+        square_of(5)
+        exp_of(5)
+        square_times_phi(5)
+        gradient(2)
+        quantise_dz(1)
+        load_g(5)
+        signed_grad(4)
+        load_z(7)
+        square_of(6)
+        exp_of(6)
+        square_times_phi(6)
+        finish(0, [sc])
+        gradient(3)
+        quantise_dz(2)
+        signed_grad(5)
+        load_g(6)
+        load_g(7)
+        square_of(7)
+        exp_of(7)
+        square_times_phi(7)
+        signed_grad(6)
+        quantise_dz(3)
+        signed_grad(7)
+        finish(1, [sc])
+        reciprocal_of(4)
+        grad_over_v(4)
+        reciprocal_of(5)
+        grad_over_v(5)
+        reciprocal_of(6)
+        grad_over_v(6)
+        reciprocal_of(7)
+        grad_over_v(7)
+        gelu_of(4)
+        gradient(4)
+        gelu_of(5)
+        gradient(5)
+        quantise_dz(4)
+        gelu_of(6)
+        gradient(6)
+        quantise_dz(5)
+        gelu_of(7)
+        gradient(7)
+        quantise_dz(6)
+        quantise_dz(7)
+        finish(2, [sc])
+        finish(3, [sc, vc])

@@ -50,7 +50,8 @@ def tile_spectralchannelmixing_v_kernel(tc, x, wc, z, grad_out, out):
         keep = pool("keep", 1)
         x_pool = pool("xs", 2)
         g_pool = pool("gs", 4)
-        z_pool = pool("z", 8)
+        z_pool = pool("z", 4)
+        gelu_pool = pool("gelu", 4)
         sq_pool = pool("sq", 4)
         exp_pool = pool("exps", 4)
         rho_pool = pool("rho", 4)
@@ -76,7 +77,7 @@ def tile_spectralchannelmixing_v_kernel(tc, x, wc, z, grad_out, out):
         x_codes = keep.tile([P, PIECES, BLOCK_CH], U32, align_bytes=64)
         x_scales = keep.tile([P, PIECES, BLOCK_CH], U8, align_bytes=64)
 
-        staged_x, staged_g, z_tiles, sq_tiles, exp_tiles, rho_tiles = {}, {}, {}, {}, {}, {}
+        staged_x, staged_g, z_tiles, gelu_tiles, sq_tiles, exp_tiles, rho_tiles = {}, {}, {}, {}, {}, {}, {}
         x_grouped, dz_grouped, dz_codes, dz_scales = {}, {}, {}, {}
 
         def piece_of(view, j):
@@ -133,9 +134,15 @@ def tile_spectralchannelmixing_v_kernel(tc, x, wc, z, grad_out, out):
             )
 
         def gelu_of(j):
+            gelu = gelu_pool.tile([P, PASS_BATCHES, ROW], F32)
             for a in range(CH_PER_PART):
-                v = channels(z_tiles[j], a)
-                nc.scalar.activation(out=v, in_=v, func=ACT.Gelu, bias=shift[:])
+                nc.scalar.activation(
+                    out=split(channels(gelu, a)),
+                    in_=sorted_tokens(channels(z_tiles[j], a)),
+                    func=ACT.Gelu,
+                    bias=shift[:],
+                )
+            gelu_tiles[j] = gelu
 
         def gp_square_of(j):
             sq = sq_pool.tile([P, PASS_BATCHES, ROW], F32)
@@ -216,13 +223,11 @@ def tile_spectralchannelmixing_v_kernel(tc, x, wc, z, grad_out, out):
                 bank = s_banks.tile([P, 4, P], F32)
                 for u in range(PASS_BATCHES):
                     for e in range(2):
-                        first = a * BATCH_TOKENS
-                        gelu = z_tiles[j][:, u, first + e : first + BATCH_TOKENS : 2]
-                        w = exp_tiles[j][:, u, first + e * P : first + (e + 1) * P]
-                        for k, term in enumerate((gelu, w)):
+                        first = a * BATCH_TOKENS + e * P
+                        for k, term in enumerate((gelu_tiles[j], exp_tiles[j])):
                             nc.tensor.matmul(
                                 out=bank[:, 2 * u + e, :],
-                                lhsT=term,
+                                lhsT=term[:, u, first : first + P],
                                 rhs=ident[:],
                                 is_transpose=True,
                                 start=(k == 0),

@@ -59,11 +59,9 @@ def tile_spectralchannelmixing_v_kernel(tc, x, wc, z, grad_out, out):
         grouped_pool = pool("grouped", 3)
         dq_pool = pool("dq", 2)
         out_pool = pool("outs", 4)
-        q_banks = ctx.enter_context(tc.psum_pool(name="q_banks", bufs=2))
-        banks = ctx.enter_context(tc.psum_pool(name="banks", bufs=2))
-        s_banks = ctx.enter_context(tc.psum_pool(name="s_banks", bufs=2))
+        banks = ctx.enter_context(tc.psum_pool(name="banks", bufs=6))
         sums = ctx.enter_context(tc.psum_pool(name="sums", bufs=2))
-        ctx.enter_context(tc.manual_schedule(engines={mybir.EngineType.Activation, mybir.EngineType.SP}))
+        ctx.enter_context(tc.manual_schedule())
 
         shift = const.tile([P, 1], F32)
         nc.vector.memset(shift[:], SHIFT)
@@ -73,6 +71,8 @@ def tile_spectralchannelmixing_v_kernel(tc, x, wc, z, grad_out, out):
         nc.scalar.activation(out=warm[:], in_=shift[:], func=ACT.Abs_reciprocal_sqrt)
         ident = const.tile([P, P], F32)
         masks.make_identity(nc, ident[:])
+        ident16 = const.tile([P, P], BF16)
+        nc.vector.tensor_copy(out=ident16[:], in_=ident[:])
 
         x_codes = keep.tile([P, PIECES, BLOCK_CH], U32, align_bytes=64)
         x_scales = keep.tile([P, PIECES, BLOCK_CH], U8, align_bytes=64)
@@ -86,12 +86,6 @@ def tile_spectralchannelmixing_v_kernel(tc, x, wc, z, grad_out, out):
 
         def channels(tile_, a):
             return tile_[:, :, a * BATCH_TOKENS : (a + 1) * BATCH_TOKENS]
-
-        def sorted_tokens(natural):
-            return natural.rearrange("q r (p e) -> q r e p", e=2)
-
-        def split(tile_):
-            return tile_.rearrange("q r (e p) -> q r e p", e=2)
 
         def load_z(j):
             z_sb = z_pool.tile([P, PASS_BATCHES, ROW], F32)
@@ -109,23 +103,23 @@ def tile_spectralchannelmixing_v_kernel(tc, x, wc, z, grad_out, out):
             nc.sync.dma_start(out=g_sb[:], in_=piece_of(g_view, j))
             staged_g[j] = g_sb
 
-        def transpose_words(staged, half):
-            words = staged[:].bitcast(F32)
-            bank = banks.tile([P, 4, P], F32)
+        def transpose_half(staged, half):
+            bank = banks.tile([P, 2, PACK, P], BF16, tag="bank")
             for a2 in range(2):
-                a = 2 * half + a2
                 for u in range(PASS_BATCHES):
-                    nc.tensor.transpose(
-                        out=bank[:, 2 * a2 + u, :], in_=words[:, u, a * P : (a + 1) * P], identity=ident[:]
-                    )
+                    for h in range(2):
+                        first = (2 * half + a2) * BATCH_TOKENS + h * P
+                        nc.tensor.transpose(
+                            out=bank[:, a2, 2 * u + h, :], in_=staged[:, u, first : first + P], identity=ident16[:]
+                        )
             return bank
 
         def lay_out_x(j, copy):
             x_g = grouped_pool.tile([P, PIECE_COLS], BF16, tag="grouped", align_bytes=64)
-            halves = x_g[:].bitcast(F32).rearrange("p (h a q u) -> p h a q u", h=2, a=2, u=2)
+            halves = x_g[:].rearrange("p (h a q t) -> p h a q t", h=2, a=2, t=PACK)
             for half in range(2):
-                bank = transpose_words(staged_x[j], half)
-                copy(out=halves[:, half], in_=bank[:].rearrange("p (a u) q -> p a q u", u=2))
+                bank = transpose_half(staged_x[j], half)
+                copy(out=halves[:, half], in_=bank[:].rearrange("p a t q -> p a q t"))
             x_grouped[j] = x_g
 
         def quantise_x(j):
@@ -137,8 +131,8 @@ def tile_spectralchannelmixing_v_kernel(tc, x, wc, z, grad_out, out):
             gelu = gelu_pool.tile([P, PASS_BATCHES, ROW], F32)
             for a in range(CH_PER_PART):
                 nc.scalar.activation(
-                    out=split(channels(gelu, a)),
-                    in_=sorted_tokens(channels(z_tiles[j], a)),
+                    out=channels(gelu, a),
+                    in_=channels(z_tiles[j], a),
                     func=ACT.Gelu,
                     bias=shift[:],
                 )
@@ -147,18 +141,14 @@ def tile_spectralchannelmixing_v_kernel(tc, x, wc, z, grad_out, out):
         def gp_square_of(j):
             sq = sq_pool.tile([P, PASS_BATCHES, ROW], F32)
             for a in range(CH_PER_PART):
-                v = sorted_tokens(channels(z_tiles[j], a))
-                nc.gpsimd.tensor_tensor(out=split(channels(sq, a)), in0=v, in1=v, op=ALU.mult)
+                v = channels(z_tiles[j], a)
+                nc.gpsimd.tensor_tensor(out=channels(sq, a), in0=v, in1=v, op=ALU.mult)
             sq_tiles[j] = sq
 
         def square_of(j):
             sq = sq_pool.tile([P, PASS_BATCHES, ROW], F32)
             for u in range(PASS_BATCHES):
-                nc.scalar.activation(
-                    out=split(sq[:, u].rearrange("q (a t) -> q a t", a=CH_PER_PART)),
-                    in_=sorted_tokens(z_tiles[j][:, u].rearrange("q (a t) -> q a t", a=CH_PER_PART)),
-                    func=ACT.Square,
-                )
+                nc.scalar.activation(out=sq[:, u], in_=z_tiles[j][:, u], func=ACT.Square)
             sq_tiles[j] = sq
 
         def signed_grad(j):
@@ -177,7 +167,7 @@ def tile_spectralchannelmixing_v_kernel(tc, x, wc, z, grad_out, out):
             rho = rho_pool.tile([P, PIECE_COLS], F32)
             by_a = rho[:].rearrange("p (a q t) -> p a q t", a=CH_PER_PART, t=PACK)
             for a in range(CH_PER_PART):
-                bank = q_banks.tile([P, 4, P], F32)
+                bank = banks.tile([P, 4, P], F32, tag="bank")
                 for u in range(PASS_BATCHES):
                     for e in range(2):
                         first = a * BATCH_TOKENS + e * P
@@ -194,13 +184,11 @@ def tile_spectralchannelmixing_v_kernel(tc, x, wc, z, grad_out, out):
             rho_tiles[j] = rho
 
         def grad_over_v(j):
-            by_a = rho_tiles[j][:].rearrange("p (a q u e) -> p a q u e", a=CH_PER_PART, u=2, e=2)
+            halves = rho_tiles[j][:].rearrange("p (h a q t) -> p h a q t", h=2, a=2, t=PACK)
             for half in range(2):
-                bank = transpose_words(staged_g[j], half)
-                signed = bank[:].bitcast(BF16).rearrange("p (a u) (q e) -> p a q u e", u=2, e=2)
-                for a2 in range(2):
-                    f = by_a[:, 2 * half + a2]
-                    nc.vector.tensor_tensor(out=f, in0=signed[:, a2], in1=f, op=ALU.mult)
+                bank = transpose_half(staged_g[j], half)
+                f = halves[:, half]
+                nc.vector.tensor_tensor(out=f, in0=bank[:].rearrange("p a t q -> p a q t"), in1=f, op=ALU.mult)
 
         def exp_of(j):
             e_t = exp_pool.tile([P, PASS_BATCHES, ROW], F32)
@@ -220,7 +208,7 @@ def tile_spectralchannelmixing_v_kernel(tc, x, wc, z, grad_out, out):
             dz_by_a = dz_g[:].rearrange("p (a q t) -> p a q t", a=CH_PER_PART, t=PACK)
             f_by_a = rho_tiles[j][:].rearrange("p (a q t) -> p a q t", a=CH_PER_PART, t=PACK)
             for a in range(CH_PER_PART):
-                bank = s_banks.tile([P, 4, P], F32)
+                bank = banks.tile([P, 4, P], F32, tag="bank")
                 for u in range(PASS_BATCHES):
                     for e in range(2):
                         first = a * BATCH_TOKENS + e * P
@@ -284,105 +272,105 @@ def tile_spectralchannelmixing_v_kernel(tc, x, wc, z, grad_out, out):
         vc, sc = nc.vector.tensor_copy, nc.scalar.copy
         load_z(0)
         load_x(0)
+        load_g(0)
         load_z(1)
+        load_x(1)
         square_of(0)
         lay_out_x(0, vc)
-        gp_square_of(1)
-        load_x(1)
-        load_g(0)
-        load_z(2)
+        square_of(1)
         reciprocal_of(0)
+        signed_grad(0)
         lay_out_x(1, vc)
         quantise_x(0)
-        signed_grad(0)
+        load_z(2)
         square_of(2)
-        reciprocal_of(1)
-        load_z(3)
-        grad_over_v(0)
         load_g(1)
-        load_x(2)
-        lay_out_x(2, vc)
-        quantise_x(1)
+        reciprocal_of(1)
         signed_grad(1)
-        gp_square_of(3)
-        reciprocal_of(2)
-        grad_over_v(1)
-        load_g(2)
+        quantise_x(1)
+        load_x(2)
         load_x(3)
+        load_z(3)
+        square_of(3)
+        reciprocal_of(2)
+        lay_out_x(2, vc)
+        grad_over_v(0)
         reciprocal_of(3)
-        signed_grad(2)
-        grad_over_v(2)
-        load_g(3)
-        signed_grad(3)
-        grad_over_v(3)
-        load_z(4)
+        load_g(2)
         lay_out_x(3, vc)
         quantise_x(2)
-        gelu_of(0)
-        gelu_of(1)
-        gelu_of(2)
-        gelu_of(3)
-        load_x(4)
-        lay_out_x(4, vc)
+        grad_over_v(1)
+        load_g(3)
         quantise_x(3)
+        signed_grad(2)
+        load_x(4)
+        load_x(5)
+        gelu_of(0)
+        signed_grad(3)
+        grad_over_v(2)
+        grad_over_v(3)
+        gelu_of(1)
+        load_z(4)
         load_z(5)
+        lay_out_x(4, vc)
+        gelu_of(2)
+        lay_out_x(5, vc)
+        quantise_x(4)
+        gelu_of(3)
+        load_z(6)
+        load_z(7)
         exp_of(0)
         square_times_phi(0)
+        load_x(6)
+        load_x(7)
+        quantise_x(5)
         exp_of(1)
         square_times_phi(1)
+        load_g(4)
         exp_of(2)
         square_times_phi(2)
+        gradient(0)
         exp_of(3)
         square_times_phi(3)
+        lay_out_x(6, vc)
+        load_g(5)
         square_of(4)
         exp_of(4)
         square_times_phi(4)
-        load_g(4)
-        load_x(5)
-        lay_out_x(5, vc)
-        quantise_x(4)
-        gradient(0)
-        load_x(6)
-        lay_out_x(6, vc)
-        quantise_x(5)
         gradient(1)
         quantise_dz(0)
-        load_x(7)
-        load_z(6)
         lay_out_x(7, vc)
         quantise_x(6)
+        load_g(6)
+        gradient(2)
+        quantise_dz(1)
         quantise_x(7)
         square_of(5)
         exp_of(5)
         square_times_phi(5)
-        gradient(2)
-        quantise_dz(1)
-        load_g(5)
+        load_g(7)
         signed_grad(4)
-        load_z(7)
+        finish(0, [vc])
         square_of(6)
         exp_of(6)
         square_times_phi(6)
-        finish(0, [sc])
         gradient(3)
         quantise_dz(2)
         signed_grad(5)
-        load_g(6)
-        load_g(7)
         square_of(7)
         exp_of(7)
         square_times_phi(7)
-        signed_grad(6)
         quantise_dz(3)
-        signed_grad(7)
-        finish(1, [sc])
         reciprocal_of(4)
-        grad_over_v(4)
         reciprocal_of(5)
-        grad_over_v(5)
+        signed_grad(6)
         reciprocal_of(6)
-        grad_over_v(6)
+        grad_over_v(4)
         reciprocal_of(7)
+        signed_grad(7)
+        grad_over_v(5)
+        finish(1, [vc])
+        grad_over_v(6)
         grad_over_v(7)
         gelu_of(4)
         gradient(4)
@@ -392,9 +380,9 @@ def tile_spectralchannelmixing_v_kernel(tc, x, wc, z, grad_out, out):
         gelu_of(6)
         gradient(6)
         quantise_dz(5)
+        finish(2, [vc])
         gelu_of(7)
         gradient(7)
         quantise_dz(6)
         quantise_dz(7)
-        finish(2, [sc])
         finish(3, [sc, vc])

@@ -192,16 +192,14 @@ def tile_spectralchannelmixing_v_kernel(tc, x, wc, z, grad_out, out):
 
         def exp_of(j):
             e_t = exp_pool.tile([P, PASS_BATCHES, ROW], F32)
-            for a in range(CH_PER_PART):
-                nc.scalar.activation(
-                    out=channels(e_t, a), in_=channels(sq_tiles[j], a), func=ACT.Exp, scale=-0.5, bias=LOG_PHI0
-                )
+            for u in range(PASS_BATCHES):
+                nc.scalar.activation(out=e_t[:, u], in_=sq_tiles[j][:, u], func=ACT.Exp, scale=-0.5, bias=LOG_PHI0)
             exp_tiles[j] = e_t
 
-        def square_times_phi(j):
-            for a in range(CH_PER_PART):
-                e_t = channels(exp_tiles[j], a)
-                nc.gpsimd.tensor_tensor(out=e_t, in0=e_t, in1=channels(sq_tiles[j], a), op=ALU.mult)
+        def square_times_phi(j, engine=nc.gpsimd):
+            for u in range(PASS_BATCHES):
+                e_t = exp_tiles[j][:, u]
+                engine.tensor_tensor(out=e_t, in0=e_t, in1=sq_tiles[j][:, u], op=ALU.mult)
 
         def gradient(j):
             dz_g = grouped_pool.tile([P, PIECE_COLS], BF16, tag="grouped", align_bytes=64)
@@ -320,46 +318,44 @@ def tile_spectralchannelmixing_v_kernel(tc, x, wc, z, grad_out, out):
         load_z(6)
         load_z(7)
         exp_of(0)
-        square_times_phi(0)
         load_x(6)
         load_x(7)
         quantise_x(5)
         exp_of(1)
-        square_times_phi(1)
         load_g(4)
         exp_of(2)
-        square_times_phi(2)
+        square_times_phi(0, nc.vector)
+        square_times_phi(1, nc.vector)
         gradient(0)
         exp_of(3)
-        square_times_phi(3)
         lay_out_x(6, vc)
         load_g(5)
         square_of(4)
         exp_of(4)
-        square_times_phi(4)
+        square_times_phi(2, nc.vector)
         gradient(1)
         quantise_dz(0)
         lay_out_x(7, vc)
         quantise_x(6)
         load_g(6)
+        square_times_phi(3, nc.vector)
         gradient(2)
         quantise_dz(1)
         quantise_x(7)
         square_of(5)
         exp_of(5)
-        square_times_phi(5)
         load_g(7)
         signed_grad(4)
         finish(0, [vc])
+        square_times_phi(4, nc.vector)
         square_of(6)
         exp_of(6)
-        square_times_phi(6)
         gradient(3)
         quantise_dz(2)
         signed_grad(5)
         square_of(7)
         exp_of(7)
-        square_times_phi(7)
+        square_times_phi(5, nc.vector)
         quantise_dz(3)
         reciprocal_of(4)
         reciprocal_of(5)
@@ -369,12 +365,14 @@ def tile_spectralchannelmixing_v_kernel(tc, x, wc, z, grad_out, out):
         reciprocal_of(7)
         signed_grad(7)
         grad_over_v(5)
-        finish(1, [vc])
         grad_over_v(6)
+        square_times_phi(6, nc.vector)
         grad_over_v(7)
+        square_times_phi(7, nc.vector)
         gelu_of(4)
         gradient(4)
         gelu_of(5)
+        finish(1, [sc])
         gradient(5)
         quantise_dz(4)
         gelu_of(6)

@@ -71,8 +71,6 @@ def tile_spectralchannelmixing_v_kernel(tc, x, wc, z, grad_out, out):
         nc.scalar.activation(out=warm[:], in_=shift[:], func=ACT.Abs_reciprocal_sqrt)
         ident = const.tile([P, P], F32)
         masks.make_identity(nc, ident[:])
-        ident16 = const.tile([P, P], BF16)
-        nc.vector.tensor_copy(out=ident16[:], in_=ident[:])
 
         x_codes = keep.tile([P, PIECES, BLOCK_CH], U32, align_bytes=64)
         x_scales = keep.tile([P, PIECES, BLOCK_CH], U8, align_bytes=64)
@@ -86,6 +84,12 @@ def tile_spectralchannelmixing_v_kernel(tc, x, wc, z, grad_out, out):
 
         def channels(tile_, a):
             return tile_[:, :, a * BATCH_TOKENS : (a + 1) * BATCH_TOKENS]
+
+        def sorted_tokens(natural):
+            return natural.rearrange("q r (p e) -> q r e p", e=2)
+
+        def split(tile_):
+            return tile_.rearrange("q r (e p) -> q r e p", e=2)
 
         def load_z(j):
             z_sb = z_pool.tile([P, PASS_BATCHES, ROW], F32)
@@ -103,23 +107,23 @@ def tile_spectralchannelmixing_v_kernel(tc, x, wc, z, grad_out, out):
             nc.sync.dma_start(out=g_sb[:], in_=piece_of(g_view, j))
             staged_g[j] = g_sb
 
-        def transpose_half(staged, half):
-            bank = banks.tile([P, 2, PACK, P], BF16, tag="bank")
+        def transpose_words(staged, half):
+            words = staged[:].bitcast(F32)
+            bank = banks.tile([P, 4, P], F32, tag="bank")
             for a2 in range(2):
+                a = 2 * half + a2
                 for u in range(PASS_BATCHES):
-                    for h in range(2):
-                        first = (2 * half + a2) * BATCH_TOKENS + h * P
-                        nc.tensor.transpose(
-                            out=bank[:, a2, 2 * u + h, :], in_=staged[:, u, first : first + P], identity=ident16[:]
-                        )
+                    nc.tensor.transpose(
+                        out=bank[:, 2 * a2 + u, :], in_=words[:, u, a * P : (a + 1) * P], identity=ident[:]
+                    )
             return bank
 
         def lay_out_x(j, copy):
             x_g = grouped_pool.tile([P, PIECE_COLS], BF16, tag="grouped", align_bytes=64)
-            halves = x_g[:].rearrange("p (h a q t) -> p h a q t", h=2, a=2, t=PACK)
+            halves = x_g[:].bitcast(F32).rearrange("p (h a q u) -> p h a q u", h=2, a=2, u=2)
             for half in range(2):
-                bank = transpose_half(staged_x[j], half)
-                copy(out=halves[:, half], in_=bank[:].rearrange("p a t q -> p a q t"))
+                bank = transpose_words(staged_x[j], half)
+                copy(out=halves[:, half], in_=bank[:].rearrange("p (a u) q -> p a q u", u=2))
             x_grouped[j] = x_g
 
         def quantise_x(j):
@@ -131,8 +135,8 @@ def tile_spectralchannelmixing_v_kernel(tc, x, wc, z, grad_out, out):
             gelu = gelu_pool.tile([P, PASS_BATCHES, ROW], F32)
             for a in range(CH_PER_PART):
                 nc.scalar.activation(
-                    out=channels(gelu, a),
-                    in_=channels(z_tiles[j], a),
+                    out=split(channels(gelu, a)),
+                    in_=sorted_tokens(channels(z_tiles[j], a)),
                     func=ACT.Gelu,
                     bias=shift[:],
                 )
@@ -141,14 +145,18 @@ def tile_spectralchannelmixing_v_kernel(tc, x, wc, z, grad_out, out):
         def gp_square_of(j):
             sq = sq_pool.tile([P, PASS_BATCHES, ROW], F32)
             for a in range(CH_PER_PART):
-                v = channels(z_tiles[j], a)
-                nc.gpsimd.tensor_tensor(out=channels(sq, a), in0=v, in1=v, op=ALU.mult)
+                v = sorted_tokens(channels(z_tiles[j], a))
+                nc.gpsimd.tensor_tensor(out=split(channels(sq, a)), in0=v, in1=v, op=ALU.mult)
             sq_tiles[j] = sq
 
         def square_of(j):
             sq = sq_pool.tile([P, PASS_BATCHES, ROW], F32)
             for u in range(PASS_BATCHES):
-                nc.scalar.activation(out=sq[:, u], in_=z_tiles[j][:, u], func=ACT.Square)
+                nc.scalar.activation(
+                    out=split(sq[:, u].rearrange("q (a t) -> q a t", a=CH_PER_PART)),
+                    in_=sorted_tokens(z_tiles[j][:, u].rearrange("q (a t) -> q a t", a=CH_PER_PART)),
+                    func=ACT.Square,
+                )
             sq_tiles[j] = sq
 
         def signed_grad(j):
@@ -184,11 +192,13 @@ def tile_spectralchannelmixing_v_kernel(tc, x, wc, z, grad_out, out):
             rho_tiles[j] = rho
 
         def grad_over_v(j):
-            halves = rho_tiles[j][:].rearrange("p (h a q t) -> p h a q t", h=2, a=2, t=PACK)
+            by_a = rho_tiles[j][:].rearrange("p (a q u e) -> p a q u e", a=CH_PER_PART, u=2, e=2)
             for half in range(2):
-                bank = transpose_half(staged_g[j], half)
-                f = halves[:, half]
-                nc.vector.tensor_tensor(out=f, in0=bank[:].rearrange("p a t q -> p a q t"), in1=f, op=ALU.mult)
+                bank = transpose_words(staged_g[j], half)
+                signed = bank[:].bitcast(BF16).rearrange("p (a u) (q e) -> p a q u e", u=2, e=2)
+                for a2 in range(2):
+                    f = by_a[:, 2 * half + a2]
+                    nc.vector.tensor_tensor(out=f, in0=signed[:, a2], in1=f, op=ALU.mult)
 
         def exp_of(j):
             e_t = exp_pool.tile([P, PASS_BATCHES, ROW], F32)

@@ -55,13 +55,13 @@ def tile_spectralchannelmixing_v_kernel(tc, x, wc, z, grad_out, out):
         sq_pool = pool("sq", 4)
         exp_pool = pool("exps", 4)
         rho_pool = pool("rho", 4)
-        sign_pool = pool("signs", 2)
+        sign_pool = pool("signs", 1)
         grouped_pool = pool("grouped", 3)
         dq_pool = pool("dq", 2)
         out_pool = pool("outs", 4)
         banks = ctx.enter_context(tc.psum_pool(name="banks", bufs=6))
         sums = ctx.enter_context(tc.psum_pool(name="sums", bufs=2))
-        ctx.enter_context(tc.manual_schedule())
+        ctx.enter_context(tc.manual_schedule(engines={mybir.EngineType.Activation, mybir.EngineType.SP}))
 
         shift = const.tile([P, 1], F32)
         nc.vector.memset(shift[:], SHIFT)
@@ -133,10 +133,10 @@ def tile_spectralchannelmixing_v_kernel(tc, x, wc, z, grad_out, out):
 
         def gelu_of(j):
             gelu = gelu_pool.tile([P, PASS_BATCHES, ROW], F32)
-            for a in range(CH_PER_PART):
+            for u in range(PASS_BATCHES):
                 nc.scalar.activation(
-                    out=split(channels(gelu, a)),
-                    in_=sorted_tokens(channels(z_tiles[j], a)),
+                    out=split(gelu[:, u].rearrange("q (a t) -> q a t", a=CH_PER_PART)),
+                    in_=sorted_tokens(z_tiles[j][:, u].rearrange("q (a t) -> q a t", a=CH_PER_PART)),
                     func=ACT.Gelu,
                     bias=shift[:],
                 )
@@ -160,20 +160,16 @@ def tile_spectralchannelmixing_v_kernel(tc, x, wc, z, grad_out, out):
             sq_tiles[j] = sq
 
         def signed_grad(j):
-            signs = []
-            for u in range(PASS_BATCHES):
-                s = sign_pool.tile([P, ROW], BF16)
-                nc.vector.tensor_scalar(
-                    out=s[:], in0=z_tiles[j][:, u], scalar1=-SHIFT, scalar2=0.5, op0=ALU.is_ge, op1=ALU.subtract
-                )
-                signs.append(s)
-            for u in range(PASS_BATCHES):
-                g = staged_g[j][:, u]
-                nc.vector.tensor_tensor(out=g, in0=g, in1=signs[u][:], op=ALU.mult)
+            s = sign_pool.tile([P, PASS_BATCHES, ROW], BF16)
+            nc.vector.tensor_scalar(
+                out=s[:], in0=z_tiles[j][:], scalar1=-SHIFT, scalar2=0.5, op0=ALU.is_ge, op1=ALU.subtract
+            )
+            g = staged_g[j]
+            nc.vector.tensor_tensor(out=g[:], in0=g[:], in1=s[:], op=ALU.mult)
 
         def reciprocal_of(j):
             rho = rho_pool.tile([P, PIECE_COLS], F32)
-            by_a = rho[:].rearrange("p (a q t) -> p a q t", a=CH_PER_PART, t=PACK)
+            by_a = rho[:].rearrange("p (a u q e) -> p a u q e", a=CH_PER_PART, u=2, e=2)
             for a in range(CH_PER_PART):
                 bank = banks.tile([P, 4, P], F32, tag="bank")
                 for u in range(PASS_BATCHES):
@@ -184,7 +180,7 @@ def tile_spectralchannelmixing_v_kernel(tc, x, wc, z, grad_out, out):
                         )
                 nc.scalar.activation(
                     out=by_a[:, a],
-                    in_=bank[:].rearrange("p t q -> p q t"),
+                    in_=bank[:].rearrange("p (u e) q -> p u q e", u=2),
                     func=ACT.Abs_reciprocal_sqrt,
                     scale=0.25,
                     bias=floor[:],
@@ -192,13 +188,12 @@ def tile_spectralchannelmixing_v_kernel(tc, x, wc, z, grad_out, out):
             rho_tiles[j] = rho
 
         def grad_over_v(j):
-            by_a = rho_tiles[j][:].rearrange("p (a q u e) -> p a q u e", a=CH_PER_PART, u=2, e=2)
+            halves = rho_tiles[j][:].rearrange("p (h n) -> p h n", h=2)
             for half in range(2):
                 bank = transpose_words(staged_g[j], half)
-                signed = bank[:].bitcast(BF16).rearrange("p (a u) (q e) -> p a q u e", u=2, e=2)
-                for a2 in range(2):
-                    f = by_a[:, 2 * half + a2]
-                    nc.vector.tensor_tensor(out=f, in0=signed[:, a2], in1=f, op=ALU.mult)
+                signed = bank[:].rearrange("p r q -> p (r q)").bitcast(BF16)
+                f = halves[:, half]
+                nc.vector.tensor_tensor(out=f, in0=signed, in1=f, op=ALU.mult)
 
         def exp_of(j):
             e_t = exp_pool.tile([P, PASS_BATCHES, ROW], F32)
@@ -213,8 +208,8 @@ def tile_spectralchannelmixing_v_kernel(tc, x, wc, z, grad_out, out):
 
         def gradient(j):
             dz_g = grouped_pool.tile([P, PIECE_COLS], BF16, tag="grouped", align_bytes=64)
-            dz_by_a = dz_g[:].rearrange("p (a q t) -> p a q t", a=CH_PER_PART, t=PACK)
-            f_by_a = rho_tiles[j][:].rearrange("p (a q t) -> p a q t", a=CH_PER_PART, t=PACK)
+            dz_by_a = dz_g[:].rearrange("p (a q u e) -> p a q u e", a=CH_PER_PART, u=2, e=2)
+            f_by_a = rho_tiles[j][:].rearrange("p (a u q e) -> p a q u e", a=CH_PER_PART, u=2, e=2)
             for a in range(CH_PER_PART):
                 bank = banks.tile([P, 4, P], F32, tag="bank")
                 for u in range(PASS_BATCHES):
@@ -230,7 +225,10 @@ def tile_spectralchannelmixing_v_kernel(tc, x, wc, z, grad_out, out):
                                 stop=(k == 1),
                             )
                 nc.vector.tensor_tensor(
-                    out=dz_by_a[:, a], in0=bank[:].rearrange("p t q -> p q t"), in1=f_by_a[:, a], op=ALU.mult
+                    out=dz_by_a[:, a],
+                    in0=bank[:].rearrange("p (u e) q -> p q u e", u=2),
+                    in1=f_by_a[:, a],
+                    op=ALU.mult,
                 )
             dz_grouped[j] = dz_g
 
@@ -305,7 +303,7 @@ def tile_spectralchannelmixing_v_kernel(tc, x, wc, z, grad_out, out):
         grad_over_v(0)
         reciprocal_of(3)
         load_g(2)
-        lay_out_x(3, vc)
+        lay_out_x(3, sc)
         quantise_x(2)
         grad_over_v(1)
         load_g(3)
@@ -322,7 +320,7 @@ def tile_spectralchannelmixing_v_kernel(tc, x, wc, z, grad_out, out):
         load_z(5)
         lay_out_x(4, vc)
         gelu_of(2)
-        lay_out_x(5, vc)
+        lay_out_x(5, sc)
         quantise_x(4)
         gelu_of(3)
         load_z(6)
@@ -345,7 +343,7 @@ def tile_spectralchannelmixing_v_kernel(tc, x, wc, z, grad_out, out):
         square_times_phi(2, nc.vector)
         gradient(1)
         quantise_dz(0)
-        lay_out_x(7, vc)
+        lay_out_x(7, sc)
         quantise_x(6)
         load_g(6)
         square_times_phi(3, nc.vector)
@@ -388,8 +386,8 @@ def tile_spectralchannelmixing_v_kernel(tc, x, wc, z, grad_out, out):
         gelu_of(6)
         gradient(6)
         quantise_dz(5)
-        finish(2, [vc])
         gelu_of(7)
+        finish(2, [sc])
         gradient(7)
         quantise_dz(6)
         quantise_dz(7)

@@ -8,6 +8,7 @@ import concourse.mybir as mybir
 F32 = mybir.dt.float32
 BF16 = mybir.dt.bfloat16
 U32 = mybir.dt.uint32
+I32 = mybir.dt.int32
 U8 = mybir.dt.uint8
 E4M3_X4 = mybir.dt.float8_e4m3fn_x4
 E5M2_X4 = mybir.dt.float8_e5m2_x4
@@ -55,10 +56,10 @@ def tile_spectralchannelmixing_v_kernel(tc, x, wc, z, grad_out, out):
         sq_pool = pool("sq", 4)
         exp_pool = pool("exps", 4)
         rho_pool = pool("rho", 4)
-        sign_pool = pool("signs", 1)
+        sign_pool = pool("signs", 3)
         grouped_pool = pool("grouped", 3)
         dq_pool = pool("dq", 2)
-        out_pool = pool("outs", 4)
+        out_pool = pool("outs", 3)
         banks = ctx.enter_context(tc.psum_pool(name="banks", bufs=6))
         sums = ctx.enter_context(tc.psum_pool(name="sums", bufs=2))
         ctx.enter_context(tc.manual_schedule(engines={mybir.EngineType.Activation, mybir.EngineType.SP}))
@@ -66,7 +67,7 @@ def tile_spectralchannelmixing_v_kernel(tc, x, wc, z, grad_out, out):
         shift = const.tile([P, 1], F32)
         nc.vector.memset(shift[:], SHIFT)
         floor = const.tile([P, 1], F32)
-        nc.vector.memset(floor[:], SHIFT * SHIFT / 4.0)
+        nc.vector.memset(floor[:], SHIFT * SHIFT)
         warm = const.tile([P, 1], F32)
         nc.scalar.activation(out=warm[:], in_=shift[:], func=ACT.Abs_reciprocal_sqrt)
         ident = const.tile([P, P], F32)
@@ -76,6 +77,7 @@ def tile_spectralchannelmixing_v_kernel(tc, x, wc, z, grad_out, out):
         x_scales = keep.tile([P, PIECES, BLOCK_CH], U8, align_bytes=64)
 
         staged_x, staged_g, z_tiles, gelu_tiles, sq_tiles, exp_tiles, rho_tiles = {}, {}, {}, {}, {}, {}, {}
+        signs = {}
         x_grouped, dz_grouped, dz_codes, dz_scales = {}, {}, {}, {}
 
         def piece_of(view, j):
@@ -159,13 +161,19 @@ def tile_spectralchannelmixing_v_kernel(tc, x, wc, z, grad_out, out):
                 )
             sq_tiles[j] = sq
 
+        def sign_of(j):
+            signs[j] = []
+            for u in range(PASS_BATCHES):
+                s = sign_pool.tile([P, ROW], BF16)
+                nc.gpsimd.tensor_scalar(
+                    out=s[:], in0=z_tiles[j][:, u], scalar1=SHIFT, scalar2=0.0, op0=ALU.add, op1=ALU.mult
+                )
+                signs[j].append(s)
+
         def signed_grad(j):
-            s = sign_pool.tile([P, PASS_BATCHES, ROW], BF16)
-            nc.vector.tensor_scalar(
-                out=s[:], in0=z_tiles[j][:], scalar1=-SHIFT, scalar2=0.5, op0=ALU.is_ge, op1=ALU.subtract
-            )
-            g = staged_g[j]
-            nc.vector.tensor_tensor(out=g[:], in0=g[:], in1=s[:], op=ALU.mult)
+            for u in range(PASS_BATCHES):
+                g = staged_g[j][:, u].bitcast(I32)
+                nc.vector.tensor_tensor(out=g, in0=g, in1=signs[j][u][:].bitcast(I32), op=ALU.bitwise_xor)
 
         def reciprocal_of(j):
             rho = rho_pool.tile([P, PIECE_COLS], F32)
@@ -182,7 +190,6 @@ def tile_spectralchannelmixing_v_kernel(tc, x, wc, z, grad_out, out):
                     out=by_a[:, a],
                     in_=bank[:].rearrange("p (u e) q -> p u q e", u=2),
                     func=ACT.Abs_reciprocal_sqrt,
-                    scale=0.25,
                     bias=floor[:],
                 )
             rho_tiles[j] = rho
@@ -210,20 +217,21 @@ def tile_spectralchannelmixing_v_kernel(tc, x, wc, z, grad_out, out):
             dz_g = grouped_pool.tile([P, PIECE_COLS], BF16, tag="grouped", align_bytes=64)
             dz_by_a = dz_g[:].rearrange("p (a q u e) -> p a q u e", a=CH_PER_PART, u=2, e=2)
             f_by_a = rho_tiles[j][:].rearrange("p (a u q e) -> p a q u e", a=CH_PER_PART, u=2, e=2)
+            terms = (gelu_tiles[j], exp_tiles[j]) if j < HALF else (exp_tiles[j], gelu_tiles[j])
             for a in range(CH_PER_PART):
                 bank = banks.tile([P, 4, P], F32, tag="bank")
-                for u in range(PASS_BATCHES):
-                    for e in range(2):
+                for k, term in enumerate(terms):
+                    for t in range(PACK):
+                        u, e = divmod(t, 2)
                         first = a * BATCH_TOKENS + e * P
-                        for k, term in enumerate((gelu_tiles[j], exp_tiles[j])):
-                            nc.tensor.matmul(
-                                out=bank[:, 2 * u + e, :],
-                                lhsT=term[:, u, first : first + P],
-                                rhs=ident[:],
-                                is_transpose=True,
-                                start=(k == 0),
-                                stop=(k == 1),
-                            )
+                        nc.tensor.matmul(
+                            out=bank[:, t, :],
+                            lhsT=term[:, u, first : first + P],
+                            rhs=ident[:],
+                            is_transpose=True,
+                            start=(k == 0 and t == 0),
+                            stop=(k == 1 and t == PACK - 1),
+                        )
                 nc.vector.tensor_tensor(
                     out=dz_by_a[:, a],
                     in0=bank[:].rearrange("p (u e) q -> p q u e", u=2),
@@ -243,7 +251,10 @@ def tile_spectralchannelmixing_v_kernel(tc, x, wc, z, grad_out, out):
             )
 
         def product(i, m):
-            acc = sums.tile([P, BLOCK_CH], F32)
+            if i < BLOCKS // 2:
+                acc = sums.tile([P, BLOCK_CH], F32)
+            else:
+                acc = banks.tile([P, BLOCK_CH], F32, tag="bank")
             rows = slice(m * P, (m + 1) * P)
             for c in range(PASSES):
                 nc.tensor.matmul_mx(
@@ -257,29 +268,37 @@ def tile_spectralchannelmixing_v_kernel(tc, x, wc, z, grad_out, out):
                 )
             return acc
 
-        def store(i, m, acc, copy):
-            result = out_pool.tile([P, BLOCK_CH], F32)
+        def store(i, m, acc, copy, result):
             copy(
-                out=result[:].rearrange("p (q a) -> p q a", a=CH_PER_PART),
+                out=result.rearrange("p (q a) -> p q a", a=CH_PER_PART),
                 in_=acc[:].rearrange("p (a q) -> p q a", a=CH_PER_PART),
             )
-            nc.sync.dma_start(out=out_view[i, m], in_=result[:])
+            nc.sync.dma_start(out=out_view[i, m], in_=result)
 
         def finish(i, copies):
+            if i >= BLOCKS // 2:
+                results = sq_pool.tile([P, CH_PER_PART, BLOCK_CH], F32, tag="sq")
+                accs = [product(i, m) for m in range(CH_PER_PART)]
+                for m in range(CH_PER_PART):
+                    store(i, m, accs[m], copies[m % len(copies)], results[:, m])
+                return
             accs = [product(i, 0)]
             for m in range(CH_PER_PART):
                 if m + 1 < CH_PER_PART:
                     accs.append(product(i, m + 1))
-                store(i, m, accs[m], copies[m % len(copies)])
+                result = out_pool.tile([P, BLOCK_CH], F32)
+                store(i, m, accs[m], copies[m % len(copies)], result[:])
 
         first_half = range(HALF)
         second_half = range(HALF, PIECES)
 
         vc, sc = nc.vector.tensor_copy, nc.scalar.copy
         load_z(0)
+        sign_of(0)
         load_x(0)
         load_g(0)
         load_z(1)
+        sign_of(1)
         load_x(1)
         square_of(0)
         lay_out_x(0, vc)
@@ -289,6 +308,7 @@ def tile_spectralchannelmixing_v_kernel(tc, x, wc, z, grad_out, out):
         lay_out_x(1, vc)
         quantise_x(0)
         load_z(2)
+        sign_of(2)
         square_of(2)
         load_g(1)
         reciprocal_of(1)
@@ -297,13 +317,14 @@ def tile_spectralchannelmixing_v_kernel(tc, x, wc, z, grad_out, out):
         load_x(2)
         load_x(3)
         load_z(3)
+        sign_of(3)
         square_of(3)
         reciprocal_of(2)
         lay_out_x(2, vc)
         grad_over_v(0)
         reciprocal_of(3)
         load_g(2)
-        lay_out_x(3, sc)
+        lay_out_x(3, vc)
         quantise_x(2)
         grad_over_v(1)
         load_g(3)
@@ -311,40 +332,45 @@ def tile_spectralchannelmixing_v_kernel(tc, x, wc, z, grad_out, out):
         signed_grad(2)
         load_x(4)
         load_x(5)
+        load_g(4)
         gelu_of(0)
         signed_grad(3)
         grad_over_v(2)
         grad_over_v(3)
         gelu_of(1)
         load_z(4)
-        load_z(5)
+        sign_of(4)
         lay_out_x(4, vc)
+        load_g(5)
         gelu_of(2)
-        lay_out_x(5, sc)
-        quantise_x(4)
-        gelu_of(3)
-        load_z(6)
-        load_z(7)
-        exp_of(0)
         load_x(6)
+        lay_out_x(5, vc)
+        quantise_x(4)
+        load_z(5)
+        sign_of(5)
         load_x(7)
+        gelu_of(3)
+        signed_grad(4)
+        lay_out_x(6, vc)
         quantise_x(5)
+        load_z(6)
+        sign_of(6)
+        load_z(7)
+        sign_of(7)
+        exp_of(0)
+        quantise_x(6)
         exp_of(1)
-        load_g(4)
         exp_of(2)
         square_times_phi(0, nc.vector)
         square_times_phi(1, nc.vector)
         gradient(0)
         exp_of(3)
-        lay_out_x(6, vc)
-        load_g(5)
         square_of(4)
         exp_of(4)
         square_times_phi(2, nc.vector)
         gradient(1)
         quantise_dz(0)
-        lay_out_x(7, sc)
-        quantise_x(6)
+        lay_out_x(7, vc)
         load_g(6)
         square_times_phi(3, nc.vector)
         gradient(2)
@@ -353,14 +379,13 @@ def tile_spectralchannelmixing_v_kernel(tc, x, wc, z, grad_out, out):
         square_of(5)
         exp_of(5)
         load_g(7)
-        signed_grad(4)
-        finish(0, [vc])
+        signed_grad(5)
         square_times_phi(4, nc.vector)
         square_of(6)
         exp_of(6)
+        finish(0, [sc])
         gradient(3)
         quantise_dz(2)
-        signed_grad(5)
         square_of(7)
         exp_of(7)
         square_times_phi(5, nc.vector)
@@ -380,15 +405,15 @@ def tile_spectralchannelmixing_v_kernel(tc, x, wc, z, grad_out, out):
         gelu_of(4)
         gradient(4)
         gelu_of(5)
-        finish(1, [sc])
+        finish(1, [sc, vc])
         gradient(5)
         quantise_dz(4)
         gelu_of(6)
         gradient(6)
         quantise_dz(5)
         gelu_of(7)
-        finish(2, [sc])
         gradient(7)
         quantise_dz(6)
+        finish(2, [sc])
         quantise_dz(7)
         finish(3, [sc, vc])

from contextlib import ExitStack

import math

import concourse.masks as masks
import concourse.mybir as mybir

F32 = mybir.dt.float32
BF16 = mybir.dt.bfloat16
U32 = mybir.dt.uint32
I32 = mybir.dt.int32
U8 = mybir.dt.uint8
E4M3_X4 = mybir.dt.float8_e4m3fn_x4
E5M2_X4 = mybir.dt.float8_e5m2_x4
ACT = mybir.ActivationFunctionType
ALU = mybir.AluOpType

P = 128
BLOCKS = 4
BLOCK_CH = 512
CH_PER_PART = BLOCK_CH // P
BATCH_TOKENS = 256
PASS_BATCHES = 2
PASSES = 2
PIECES = BLOCKS * PASSES
ROW = CH_PER_PART * BATCH_TOKENS
PACK = 4
PIECE_COLS = PACK * BLOCK_CH
HALF = PIECES // 2

SHIFT = 2.0**-56
LOG_PHI0 = -0.5 * math.log(2.0 * math.pi)

FLOPS = 2 * BLOCKS * BLOCK_CH * BLOCK_CH * PASSES * PASS_BATCHES * BATCH_TOKENS
BYTES = BLOCKS * BLOCK_CH * 1024 * (2 + 4 + 2) + BLOCKS * BLOCK_CH * BLOCK_CH * 4


def tile_spectralchannelmixing_v_kernel(tc, x, wc, z, grad_out, out):
    nc = tc.nc
    by_piece = "b (i q a) h w -> i q b (a h w)"
    x_view = x.rearrange(by_piece, i=BLOCKS, q=P, a=CH_PER_PART)
    z_view = z.rearrange(by_piece, i=BLOCKS, q=P, a=CH_PER_PART)
    g_view = grad_out.rearrange(by_piece, i=BLOCKS, q=P, a=CH_PER_PART)
    out_view = out.rearrange("i (q a) k -> i a q k", a=CH_PER_PART)

    with ExitStack() as ctx:
        def pool(name, bufs):
            return ctx.enter_context(tc.tile_pool(name=name, bufs=bufs))

        const = pool("const", 1)
        keep = pool("keep", 1)
        x_pool = pool("xs", 2)
        g_pool = pool("gs", 4)
        z_pool = pool("z", 4)
        gelu_pool = pool("gelu", 4)
        sq_pool = pool("sq", 4)
        exp_pool = pool("exps", 4)
        rho_pool = pool("rho", 4)
        sign_pool = pool("signs", 3)
        grouped_pool = pool("grouped", 3)
        dq_pool = pool("dq", 2)
        out_pool = pool("outs", 3)
        banks = ctx.enter_context(tc.psum_pool(name="banks", bufs=6))
        sums = ctx.enter_context(tc.psum_pool(name="sums", bufs=2))
        ctx.enter_context(tc.manual_schedule(engines={mybir.EngineType.Activation, mybir.EngineType.SP}))

        shift = const.tile([P, 1], F32)
        nc.vector.memset(shift[:], SHIFT)
        floor = const.tile([P, 1], F32)
        nc.vector.memset(floor[:], SHIFT * SHIFT)
        warm = const.tile([P, 1], F32)
        nc.scalar.activation(out=warm[:], in_=shift[:], func=ACT.Abs_reciprocal_sqrt)
        ident = const.tile([P, P], F32)
        masks.make_identity(nc, ident[:])

        x_codes = keep.tile([P, PIECES, BLOCK_CH], U32, align_bytes=64)
        x_scales = keep.tile([P, PIECES, BLOCK_CH], U8, align_bytes=64)

        staged_x, staged_g, z_tiles, gelu_tiles, sq_tiles, exp_tiles, rho_tiles = {}, {}, {}, {}, {}, {}, {}
        signs = {}
        x_grouped, dz_grouped, dz_codes, dz_scales = {}, {}, {}, {}

        def piece_of(view, j):
            first = PASS_BATCHES * (j % PASSES)
            return view[j // PASSES, :, first : first + PASS_BATCHES, :]

        def channels(tile_, a):
            return tile_[:, :, a * BATCH_TOKENS : (a + 1) * BATCH_TOKENS]

        def sorted_tokens(natural):
            return natural.rearrange("q r (p e) -> q r e p", e=2)

        def split(tile_):
            return tile_.rearrange("q r (e p) -> q r e p", e=2)

        def load_z(j):
            z_sb = z_pool.tile([P, PASS_BATCHES, ROW], F32)
            for u in range(PASS_BATCHES):
                nc.sync.dma_start(out=z_sb[:, u], in_=piece_of(z_view, j)[:, u])
            z_tiles[j] = z_sb

        def load_x(j):
            x_sb = x_pool.tile([P, PASS_BATCHES, ROW], BF16)
            nc.sync.dma_start(out=x_sb[:], in_=piece_of(x_view, j))
            staged_x[j] = x_sb

        def load_g(j):
            g_sb = g_pool.tile([P, PASS_BATCHES, ROW], BF16)
            nc.sync.dma_start(out=g_sb[:], in_=piece_of(g_view, j))
            staged_g[j] = g_sb

        def transpose_words(staged, half):
            words = staged[:].bitcast(F32)
            bank = banks.tile([P, 4, P], F32, tag="bank")
            for a2 in range(2):
                a = 2 * half + a2
                for u in range(PASS_BATCHES):
                    nc.tensor.transpose(
                        out=bank[:, 2 * a2 + u, :], in_=words[:, u, a * P : (a + 1) * P], identity=ident[:]
                    )
            return bank

        def lay_out_x(j, copy):
            x_g = grouped_pool.tile([P, PIECE_COLS], BF16, tag="grouped", align_bytes=64)
            halves = x_g[:].bitcast(F32).rearrange("p (h a q u) -> p h a q u", h=2, a=2, u=2)
            for half in range(2):
                bank = transpose_words(staged_x[j], half)
                copy(out=halves[:, half], in_=bank[:].rearrange("p (a u) q -> p a q u", u=2))
            x_grouped[j] = x_g

        def quantise_x(j):
            nc.vector.quantize_mx(
                out=x_codes[:, j, :].bitcast(E4M3_X4), scales=x_scales[:, j, :], in_=x_grouped[j][:]
            )

        def gelu_of(j):
            gelu = gelu_pool.tile([P, PASS_BATCHES, ROW], F32)
            for u in range(PASS_BATCHES):
                nc.scalar.activation(
                    out=split(gelu[:, u].rearrange("q (a t) -> q a t", a=CH_PER_PART)),
                    in_=sorted_tokens(z_tiles[j][:, u].rearrange("q (a t) -> q a t", a=CH_PER_PART)),
                    func=ACT.Gelu,
                    bias=shift[:],
                )
            gelu_tiles[j] = gelu

        def gp_square_of(j):
            sq = sq_pool.tile([P, PASS_BATCHES, ROW], F32)
            for a in range(CH_PER_PART):
                v = sorted_tokens(channels(z_tiles[j], a))
                nc.gpsimd.tensor_tensor(out=split(channels(sq, a)), in0=v, in1=v, op=ALU.mult)
            sq_tiles[j] = sq

        def square_of(j):
            sq = sq_pool.tile([P, PASS_BATCHES, ROW], F32)
            for u in range(PASS_BATCHES):
                nc.scalar.activation(
                    out=split(sq[:, u].rearrange("q (a t) -> q a t", a=CH_PER_PART)),
                    in_=sorted_tokens(z_tiles[j][:, u].rearrange("q (a t) -> q a t", a=CH_PER_PART)),
                    func=ACT.Square,
                )
            sq_tiles[j] = sq

        def sign_of(j):
            signs[j] = []
            for u in range(PASS_BATCHES):
                s = sign_pool.tile([P, ROW], BF16)
                nc.gpsimd.tensor_scalar(
                    out=s[:], in0=z_tiles[j][:, u], scalar1=SHIFT, scalar2=0.0, op0=ALU.add, op1=ALU.mult
                )
                signs[j].append(s)

        def signed_grad(j):
            for u in range(PASS_BATCHES):
                g = staged_g[j][:, u].bitcast(I32)
                nc.vector.tensor_tensor(out=g, in0=g, in1=signs[j][u][:].bitcast(I32), op=ALU.bitwise_xor)

        def reciprocal_of(j):
            rho = rho_pool.tile([P, PIECE_COLS], F32)
            by_a = rho[:].rearrange("p (a u q e) -> p a u q e", a=CH_PER_PART, u=2, e=2)
            for a in range(CH_PER_PART):
                bank = banks.tile([P, 4, P], F32, tag="bank")
                for u in range(PASS_BATCHES):
                    for e in range(2):
                        first = a * BATCH_TOKENS + e * P
                        nc.tensor.transpose(
                            out=bank[:, 2 * u + e, :], in_=sq_tiles[j][:, u, first : first + P], identity=ident[:]
                        )
                nc.scalar.activation(
                    out=by_a[:, a],
                    in_=bank[:].rearrange("p (u e) q -> p u q e", u=2),
                    func=ACT.Abs_reciprocal_sqrt,
                    bias=floor[:],
                )
            rho_tiles[j] = rho

        def grad_over_v(j):
            halves = rho_tiles[j][:].rearrange("p (h n) -> p h n", h=2)
            for half in range(2):
                bank = transpose_words(staged_g[j], half)
                signed = bank[:].rearrange("p r q -> p (r q)").bitcast(BF16)
                f = halves[:, half]
                nc.vector.tensor_tensor(out=f, in0=signed, in1=f, op=ALU.mult)

        def exp_of(j):
            e_t = exp_pool.tile([P, PASS_BATCHES, ROW], F32)
            for u in range(PASS_BATCHES):
                nc.scalar.activation(out=e_t[:, u], in_=sq_tiles[j][:, u], func=ACT.Exp, scale=-0.5, bias=LOG_PHI0)
            exp_tiles[j] = e_t

        def square_times_phi(j, engine=nc.gpsimd):
            for u in range(PASS_BATCHES):
                e_t = exp_tiles[j][:, u]
                engine.tensor_tensor(out=e_t, in0=e_t, in1=sq_tiles[j][:, u], op=ALU.mult)

        def gradient(j):
            dz_g = grouped_pool.tile([P, PIECE_COLS], BF16, tag="grouped", align_bytes=64)
            dz_by_a = dz_g[:].rearrange("p (a q u e) -> p a q u e", a=CH_PER_PART, u=2, e=2)
            f_by_a = rho_tiles[j][:].rearrange("p (a u q e) -> p a q u e", a=CH_PER_PART, u=2, e=2)
            terms = (gelu_tiles[j], exp_tiles[j]) if j < HALF else (exp_tiles[j], gelu_tiles[j])
            for a in range(CH_PER_PART):
                bank = banks.tile([P, 4, P], F32, tag="bank")
                for k, term in enumerate(terms):
                    for t in range(PACK):
                        u, e = divmod(t, 2)
                        first = a * BATCH_TOKENS + e * P
                        nc.tensor.matmul(
                            out=bank[:, t, :],
                            lhsT=term[:, u, first : first + P],
                            rhs=ident[:],
                            is_transpose=True,
                            start=(k == 0 and t == 0),
                            stop=(k == 1 and t == PACK - 1),
                        )
                nc.vector.tensor_tensor(
                    out=dz_by_a[:, a],
                    in0=bank[:].rearrange("p (u e) q -> p q u e", u=2),
                    in1=f_by_a[:, a],
                    op=ALU.mult,
                )
            dz_grouped[j] = dz_g

        def quantise_dz(j):
            i, c = divmod(j, PASSES)
            if c == 0:
                codes = dq_pool.tile([P, PASSES, BLOCK_CH], U32, align_bytes=64)
                scales = dq_pool.tile([P, PASSES, BLOCK_CH], U8, align_bytes=64)
                dz_codes[i], dz_scales[i] = codes, scales
            nc.vector.quantize_mx(
                out=dz_codes[i][:, c, :].bitcast(E5M2_X4), scales=dz_scales[i][:, c, :], in_=dz_grouped[j][:]
            )

        def product(i, m):
            if i < BLOCKS // 2:
                acc = sums.tile([P, BLOCK_CH], F32)
            else:
                acc = banks.tile([P, BLOCK_CH], F32, tag="bank")
            rows = slice(m * P, (m + 1) * P)
            for c in range(PASSES):
                nc.tensor.matmul_mx(
                    out=acc[:],
                    lhsT=x_codes[:, PASSES * i + c, rows].bitcast(E4M3_X4),
                    lhsT_scale=x_scales[:, PASSES * i + c, rows],
                    rhs=dz_codes[i][:, c, :].bitcast(E5M2_X4),
                    rhs_scale=dz_scales[i][:, c, :],
                    start=(c == 0),
                    stop=(c == PASSES - 1),
                )
            return acc

        def store(i, m, acc, copy, result):
            copy(
                out=result.rearrange("p (q a) -> p q a", a=CH_PER_PART),
                in_=acc[:].rearrange("p (a q) -> p q a", a=CH_PER_PART),
            )
            nc.sync.dma_start(out=out_view[i, m], in_=result)

        def finish(i, copies):
            if i >= BLOCKS // 2:
                results = sq_pool.tile([P, CH_PER_PART, BLOCK_CH], F32, tag="sq")
                accs = [product(i, m) for m in range(CH_PER_PART)]
                for m in range(CH_PER_PART):
                    store(i, m, accs[m], copies[m % len(copies)], results[:, m])
                return
            accs = [product(i, 0)]
            for m in range(CH_PER_PART):
                if m + 1 < CH_PER_PART:
                    accs.append(product(i, m + 1))
                result = out_pool.tile([P, BLOCK_CH], F32)
                store(i, m, accs[m], copies[m % len(copies)], result[:])

        first_half = range(HALF)
        second_half = range(HALF, PIECES)

        vc, sc = nc.vector.tensor_copy, nc.scalar.copy
        load_z(0)
        sign_of(0)
        load_x(0)
        load_g(0)
        load_z(1)
        sign_of(1)
        load_x(1)
        square_of(0)
        lay_out_x(0, vc)
        square_of(1)
        reciprocal_of(0)
        signed_grad(0)
        lay_out_x(1, vc)
        quantise_x(0)
        load_z(2)
        sign_of(2)
        square_of(2)
        load_g(1)
        reciprocal_of(1)
        signed_grad(1)
        quantise_x(1)
        load_x(2)
        load_x(3)
        load_z(3)
        sign_of(3)
        square_of(3)
        reciprocal_of(2)
        lay_out_x(2, vc)
        grad_over_v(0)
        reciprocal_of(3)
        load_g(2)
        lay_out_x(3, vc)
        quantise_x(2)
        grad_over_v(1)
        load_g(3)
        quantise_x(3)
        signed_grad(2)
        load_x(4)
        load_x(5)
        load_g(4)
        gelu_of(0)
        signed_grad(3)
        grad_over_v(2)
        grad_over_v(3)
        gelu_of(1)
        load_z(4)
        sign_of(4)
        lay_out_x(4, vc)
        load_g(5)
        gelu_of(2)
        load_x(6)
        lay_out_x(5, vc)
        quantise_x(4)
        load_z(5)
        sign_of(5)
        load_x(7)
        gelu_of(3)
        signed_grad(4)
        lay_out_x(6, vc)
        quantise_x(5)
        load_z(6)
        sign_of(6)
        load_z(7)
        sign_of(7)
        exp_of(0)
        quantise_x(6)
        exp_of(1)
        exp_of(2)
        square_times_phi(0, nc.vector)
        square_times_phi(1, nc.vector)
        gradient(0)
        exp_of(3)
        square_of(4)
        exp_of(4)
        square_times_phi(2, nc.vector)
        gradient(1)
        quantise_dz(0)
        lay_out_x(7, vc)
        load_g(6)
        square_times_phi(3, nc.vector)
        gradient(2)
        quantise_dz(1)
        quantise_x(7)
        square_of(5)
        exp_of(5)
        load_g(7)
        signed_grad(5)
        square_times_phi(4, nc.vector)
        square_of(6)
        exp_of(6)
        finish(0, [sc])
        gradient(3)
        quantise_dz(2)
        square_of(7)
        exp_of(7)
        square_times_phi(5, nc.vector)
        quantise_dz(3)
        reciprocal_of(4)
        reciprocal_of(5)
        signed_grad(6)
        reciprocal_of(6)
        grad_over_v(4)
        reciprocal_of(7)
        signed_grad(7)
        grad_over_v(5)
        grad_over_v(6)
        square_times_phi(6, nc.vector)
        grad_over_v(7)
        square_times_phi(7, nc.vector)
        gelu_of(4)
        gradient(4)
        gelu_of(5)
        finish(1, [sc, vc])
        gradient(5)
        quantise_dz(4)
        gelu_of(6)
        gradient(6)
        quantise_dz(5)
        gelu_of(7)
        gradient(7)
        quantise_dz(6)
        finish(2, [sc])
        quantise_dz(7)
        finish(3, [sc, vc])
